import numpy as np
import ml_dtypes


def mxq(x, axis, fmt="e4m3"):
    dtype, down = {"e4m3": (ml_dtypes.float8_e4m3fn, 7), "e5m2": (ml_dtypes.float8_e5m2, 14)}[fmt]
    v = np.moveaxis(np.asarray(x, np.float32).astype(ml_dtypes.bfloat16).astype(np.float64), axis, -1)
    blocks = v.reshape(v.shape[:-1] + (-1, 32))
    amax = np.abs(blocks).max(-1, keepdims=True)
    byte = np.maximum(np.where(amax > 0, np.frexp(amax)[1] - 1 + 127, 0) - down, 1)
    scale = np.exp2(byte - 127.0)
    codes = (blocks / scale).astype(np.float32).astype(dtype).astype(np.float64)
    return np.moveaxis((codes * scale).reshape(v.shape), -1, axis)


WIDE = False


def mx_kscale(k):
    if not WIDE:
        return np.ones(k)
    levels = np.array([10, -10, 5, -5, 0])
    a = np.random.permutation(np.resize(levels, k // 512 * 4)).reshape(k // 512, 4)
    idx = np.arange(k)
    return np.exp2(a[idx // 512, idx % 128 // 32])


BF16 = ml_dtypes.bfloat16


def bf(x):
    return np.asarray(x, np.float32).astype(BF16)


def f64(x):
    return np.asarray(x).astype(np.float64)


B, S, D_IN, D_OUT, GROUP_SIZE = 4, 256, 1024, 4096, 128
EPS = 1e-8


def group_kscale(k, g):
    u = np.unique(mx_kscale(k))
    n = len(u)
    lv = u[[n - 1 - i // 2 if i % 2 == 0 else i // 2 for i in range(n)]]
    return np.repeat(lv[np.arange(k // g) % n], g)


def ternary_quantize_groupwise(w, group_size=GROUP_SIZE, eps=EPS):
    orig_shape = w.shape
    last = orig_shape[-1]
    pad = (-last) % group_size
    if pad > 0:
        w = np.pad(w, [(0, 0)] * (w.ndim - 1) + [(0, pad)])
    num_groups = w.shape[-1] // group_size
    wg = w.reshape(-1, num_groups, group_size)
    scale = np.maximum(np.mean(np.abs(wg), axis=-1, keepdims=True), eps)
    wn = wg / scale
    q = np.where(wn > 0.5, 1.0, np.where(wn < -0.5, -1.0, 0.0))
    wq = (q * scale).reshape(w.shape)
    if pad > 0:
        wq = wq[..., :last]
    return wq.reshape(orig_shape)


def quantize_with_ste(w_real, group_size=GROUP_SIZE):
    w_q = ternary_quantize_groupwise(w_real, group_size=group_size)
    return w_real + (w_q - w_real)


def setup_inputs():
    s = group_kscale(D_IN, GROUP_SIZE)
    bound_w = 2.0 / np.sqrt(D_IN)
    return {"x": bf(np.random.standard_normal((B, S, D_IN)) * s),
            "weight": bf(np.random.uniform(-bound_w, bound_w, (D_OUT, D_IN)) / s),
            "bias": bf(np.random.uniform(-0.5, 0.5, D_OUT))}


def reference(x, weight, bias):
    w_q = quantize_with_ste(f64(weight), group_size=GROUP_SIZE)
    return (mxq(f64(x), 2, "e4m3") @ mxq(w_q, 1, "e4m3").T) + f64(bias)

@@ -1,0 +1,204 @@
+from contextlib import ExitStack
+
+import concourse.mybir as mybir
+from concourse.masks import make_identity
+
+F32 = mybir.dt.float32
+BF16 = mybir.dt.bfloat16
+U32 = mybir.dt.uint32
+U8 = mybir.dt.uint8
+FP8X4 = mybir.dt.float8_e4m3fn_x4
+ALU = mybir.AluOpType
+ACT = mybir.ActivationFunctionType
+
+P = 128
+TOK = 1024
+K = 1024
+OUT = 4096
+GROUP = 128
+EPS = 1e-8
+NB = 512
+NBLK = OUT // NB
+A_T = NB // P
+G = K // GROUP
+MT = TOK // P
+C = K // 512
+
+FLOPS = 2 * TOK * K * OUT
+
+
+def tile_bitlinear_kernel(tc, x, weight, bias, out):
+    nc = tc.nc
+    xf = x.flatten_outer_dims()
+    of = out.flatten_outer_dims()
+    with ExitStack() as ctx:
+        const = ctx.enter_context(tc.tile_pool(name="const", bufs=1))
+        wpool = ctx.enter_context(tc.tile_pool(name="wpool", bufs=NBLK))
+        work = ctx.enter_context(tc.tile_pool(name="work", bufs=2))
+        small = ctx.enter_context(tc.tile_pool(name="small", bufs=3))
+        codes = ctx.enter_context(tc.tile_pool(name="codes", bufs=3))
+        outp = ctx.enter_context(tc.tile_pool(name="outp", bufs=6))
+        psum_t = ctx.enter_context(tc.psum_pool(name="psum_t", bufs=3))
+        psum_a = ctx.enter_context(tc.psum_pool(name="psum_a", bufs=4))
+
+        w_sb = []
+
+        def load_w(n):
+            w_n = wpool.tile([P, A_T, K], BF16, name="w_n", tag="w_n")
+            nc.sync.dma_start(
+                out=w_n[:],
+                in_=weight[n * NB : (n + 1) * NB, :].rearrange("(a p) k -> p a k", p=P),
+            )
+            w_sb.append(w_n)
+
+        load_w(0)
+        x_sb = const.tile([P, MT, K], BF16, name="x_sb")
+        nc.sync.dma_start(out=x_sb[:], in_=xf.rearrange("(m p) k -> p m k", p=P))
+        load_w(1)
+        bias_bc = const.tile([P, OUT], BF16, name="bias_bc")
+        nc.sync.dma_start(out=bias_bc[:], in_=bias.partition_broadcast(P))
+        for n in range(2, NBLK):
+            load_w(n)
+
+        ident_f = const.tile([P, P], F32, name="ident_f")
+        make_identity(nc, ident_f[:])
+        ident_b = const.tile([P, P], BF16, name="ident_b")
+        make_identity(nc, ident_b[:])
+
+        xg = const.tile([P, C, TOK, 4], BF16, name="xg", align_bytes=64)
+        x_codes = const.tile([P, C, TOK], U32, name="x_codes", align_bytes=64)
+        x_scales = const.tile([P, C, TOK], U8, name="x_scales", align_bytes=64)
+
+        state = {}
+
+        def stage_sums(n):
+            sums = small.tile([P, A_T * G], F32, name="sums", tag="sums")
+            absw = work.tile([P, A_T, K], BF16, name="absw", tag="absw")
+            for a in range(A_T):
+                for g in range(G):
+                    j = a * G + g
+                    nc.scalar.activation(
+                        out=absw[:, a, g * GROUP : (g + 1) * GROUP],
+                        in_=w_sb[n][:, a, g * GROUP : (g + 1) * GROUP],
+                        func=ACT.Abs,
+                        accum_out=sums[:, j : j + 1],
+                    )
+            state[("sums", n)] = sums
+            state[("absw", n)] = absw
+
+        def stage_ternary(n):
+            sums = state[("sums", n)]
+            absw = state[("absw", n)]
+            thr = small.tile([P, A_T * G], F32, name="thr", tag="thr")
+            s2 = small.tile([P, A_T * G], F32, name="s2", tag="s2")
+            nc.vector.tensor_scalar(
+                out=thr[:], in0=sums[:], scalar1=1.0 / 256.0, scalar2=EPS / 2.0,
+                op0=ALU.mult, op1=ALU.max,
+            )
+            nc.vector.tensor_scalar(
+                out=s2[:], in0=sums[:], scalar1=1.0 / 64.0, scalar2=EPS * 2.0,
+                op0=ALU.mult, op1=ALU.max,
+            )
+            sg = work.tile([P, A_T, K], BF16, name="sg", tag="sg")
+            nc.vector.tensor_scalar(
+                out=sg[:], in0=w_sb[n][:], scalar1=0.0, scalar2=0.5,
+                op0=ALU.is_ge, op1=ALU.subtract,
+            )
+            for a in range(A_T):
+                for g in range(G):
+                    j = a * G + g
+                    sl = absw[:, a, g * GROUP : (g + 1) * GROUP]
+                    nc.vector.tensor_scalar(
+                        out=sl, in0=sl, scalar1=thr[:, j : j + 1], scalar2=s2[:, j : j + 1],
+                        op0=ALU.is_gt, op1=ALU.mult,
+                    )
+                nc.vector.tensor_tensor(
+                    out=sg[:, a, :], in0=absw[:, a, :], in1=sg[:, a, :], op=ALU.mult
+                )
+            state[("wq", n)] = sg
+
+        def stage_transpose(n):
+            wq = state[("wq", n)]
+            grouped = work.tile([P, C, NB, 4], BF16, name="grouped", tag="grouped", align_bytes=64)
+            for a in range(A_T):
+                ps = psum_t.tile([P, C, 4, P], BF16, name="ps_w", tag="tp")
+                view = wq[:, a, :].rearrange("p (c q t) -> p c t q", c=C, t=4)
+                for c in range(C):
+                    for t in range(4):
+                        nc.tensor.transpose(ps[:, c, t, :], view[:, c, t, :], ident_b[:])
+                nc.scalar.copy(
+                    out=grouped[:, :, a * P : (a + 1) * P, :],
+                    in_=ps[:].rearrange("p c t o -> p c o t"),
+                )
+            state[("grouped", n)] = grouped
+
+        def stage_quant(n):
+            grouped = state[("grouped", n)]
+            w_codes = codes.tile([P, C, NB], U32, name="w_codes", tag="w_codes", align_bytes=64)
+            w_scales = codes.tile([P, C, NB], U8, name="w_scales", tag="w_scales", align_bytes=64)
+            for c in range(C):
+                nc.vector.quantize_mx(
+                    out=w_codes[:, c, :].bitcast(FP8X4),
+                    scales=w_scales[:, c, :],
+                    in_=grouped[:, c, :, :].rearrange("p o t -> p (o t)"),
+                )
+            state[("codes", n)] = (w_codes, w_scales)
+
+        def stage_mm(n):
+            w_codes, w_scales = state[("codes", n)]
+            for m in range(MT):
+                acc = psum_a.tile([P, NB], F32, name="acc", tag="acc")
+                for c in range(C):
+                    nc.tensor.matmul_mx(
+                        out=acc[:],
+                        lhsT=x_codes[:, c, m * P : (m + 1) * P].bitcast(FP8X4),
+                        lhsT_scale=x_scales[:, c, m * P : (m + 1) * P],
+                        rhs=w_codes[:, c, :].bitcast(FP8X4),
+                        rhs_scale=w_scales[:, c, :],
+                        start=(c == 0),
+                        stop=(c == C - 1),
+                    )
+                o_sb = outp.tile([P, NB], F32, name="o_sb", tag="o_sb")
+                nc.vector.tensor_tensor(
+                    out=o_sb[:], in0=acc[:], in1=bias_bc[:, n * NB : (n + 1) * NB], op=ALU.add
+                )
+                nc.sync.dma_start(
+                    out=of[m * P : (m + 1) * P, n * NB : (n + 1) * NB], in_=o_sb[:]
+                )
+
+        def stage_x():
+            xw = x_sb[:].bitcast(F32).rearrange("p m (c q u) -> p m c u q", c=C, u=2)
+            xg32 = xg[:].bitcast(F32)
+            for m in range(MT):
+                ps = psum_t.tile([P, C, 2, P], F32, name="ps_x", tag="tp")
+                for c in range(C):
+                    for u in range(2):
+                        nc.tensor.transpose(ps[:, c, u, :], xw[:, m, c, u, :], ident_f[:])
+                nc.vector.tensor_copy(
+                    out=xg32[:, :, m * P : (m + 1) * P, :],
+                    in_=ps[:].rearrange("p c u k -> p c k u"),
+                )
+            for c in range(C):
+                for h in range(2):
+                    sl = slice(h * 512, (h + 1) * 512)
+                    nc.vector.quantize_mx(
+                        out=x_codes[:, c, sl].bitcast(FP8X4),
+                        scales=x_scales[:, c, sl],
+                        in_=xg[:, c, sl, :].rearrange("p k t -> p (k t)"),
+                    )
+
+        stage_sums(0)
+        stage_x()
+        stage_ternary(0)
+        stage_sums(1)
+        stage_transpose(0)
+        stage_quant(0)
+        for n in range(NBLK):
+            if n + 1 < NBLK:
+                stage_ternary(n + 1)
+            if n + 2 < NBLK:
+                stage_sums(n + 2)
+            stage_mm(n)
+            if n + 1 < NBLK:
+                stage_transpose(n + 1)
+                stage_quant(n + 1)

@@ -126,10 +126,16 @@ def tile_bitlinear_kernel(tc, x, weight, bias, out):
                 for c in range(C):
                     for t in range(4):
                         nc.tensor.transpose(ps[:, c, t, :], view[:, c, t, :], ident_b[:])
-                nc.scalar.copy(
-                    out=grouped[:, :, a * P : (a + 1) * P, :],
-                    in_=ps[:].rearrange("p c t o -> p c o t"),
-                )
+                if a == A_T - 1:
+                    nc.vector.tensor_copy(
+                        out=grouped[:, :, a * P : (a + 1) * P, :],
+                        in_=ps[:].rearrange("p c t o -> p c o t"),
+                    )
+                else:
+                    nc.scalar.copy(
+                        out=grouped[:, :, a * P : (a + 1) * P, :],
+                        in_=ps[:].rearrange("p c t o -> p c o t"),
+                    )
             state[("grouped", n)] = grouped
 
         def stage_quant(n):

@@ -23,6 +23,7 @@ A_T = NB // P
 G = K // GROUP
 MT = TOK // P
 C = K // 512
+SIGN_ON_SCALAR = (2, 5)
 
 FLOPS = 2 * TOK * K * OUT
 
@@ -95,15 +96,19 @@ def tile_bitlinear_kernel(tc, x, weight, bias, out):
                 out=thr[:], in0=sums[:], scalar1=1.0 / 256.0, scalar2=EPS / 2.0,
                 op0=ALU.mult, op1=ALU.max,
             )
+            f = 1.0 if n in SIGN_ON_SCALAR else 2.0
             nc.vector.tensor_scalar(
-                out=s2[:], in0=sums[:], scalar1=1.0 / 64.0, scalar2=EPS * 2.0,
+                out=s2[:], in0=sums[:], scalar1=f / 128.0, scalar2=EPS * f,
                 op0=ALU.mult, op1=ALU.max,
             )
             sg = work.tile([P, A_T, K], BF16, name="sg", tag="sg")
-            nc.vector.tensor_scalar(
-                out=sg[:], in0=w_sb[n][:], scalar1=0.0, scalar2=0.5,
-                op0=ALU.is_ge, op1=ALU.subtract,
-            )
+            if n in SIGN_ON_SCALAR:
+                nc.scalar.activation(out=sg[:], in_=w_sb[n][:], func=ACT.Sign)
+            else:
+                nc.vector.tensor_scalar(
+                    out=sg[:], in0=w_sb[n][:], scalar1=0.0, scalar2=0.5,
+                    op0=ALU.is_ge, op1=ALU.subtract,
+                )
             for a in range(A_T):
                 for g in range(G):
                     j = a * G + g
@@ -126,16 +131,10 @@ def tile_bitlinear_kernel(tc, x, weight, bias, out):
                 for c in range(C):
                     for t in range(4):
                         nc.tensor.transpose(ps[:, c, t, :], view[:, c, t, :], ident_b[:])
-                if a == A_T - 1:
-                    nc.vector.tensor_copy(
-                        out=grouped[:, :, a * P : (a + 1) * P, :],
-                        in_=ps[:].rearrange("p c t o -> p c o t"),
-                    )
-                else:
-                    nc.scalar.copy(
-                        out=grouped[:, :, a * P : (a + 1) * P, :],
-                        in_=ps[:].rearrange("p c t o -> p c o t"),
-                    )
+                nc.scalar.copy(
+                    out=grouped[:, :, a * P : (a + 1) * P, :],
+                    in_=ps[:].rearrange("p c t o -> p c o t"),
+                )
             state[("grouped", n)] = grouped
 
         def stage_quant(n):
@@ -180,7 +179,7 @@ def tile_bitlinear_kernel(tc, x, weight, bias, out):
                 for c in range(C):
                     for u in range(2):
                         nc.tensor.transpose(ps[:, c, u, :], xw[:, m, c, u, :], ident_f[:])
-                nc.vector.tensor_copy(
+                nc.scalar.copy(
                     out=xg32[:, :, m * P : (m + 1) * P, :],
                     in_=ps[:].rearrange("p c u k -> p c k u"),
                 )

@@ -23,7 +23,7 @@ A_T = NB // P
 G = K // GROUP
 MT = TOK // P
 C = K // 512
-SIGN_ON_SCALAR = (2, 5)
+BIAS_ON_GPSIMD = (7,)
 
 FLOPS = 2 * TOK * K * OUT
 
@@ -96,19 +96,15 @@ def tile_bitlinear_kernel(tc, x, weight, bias, out):
                 out=thr[:], in0=sums[:], scalar1=1.0 / 256.0, scalar2=EPS / 2.0,
                 op0=ALU.mult, op1=ALU.max,
             )
-            f = 1.0 if n in SIGN_ON_SCALAR else 2.0
             nc.vector.tensor_scalar(
-                out=s2[:], in0=sums[:], scalar1=f / 128.0, scalar2=EPS * f,
+                out=s2[:], in0=sums[:], scalar1=1.0 / 64.0, scalar2=EPS * 2.0,
                 op0=ALU.mult, op1=ALU.max,
             )
             sg = work.tile([P, A_T, K], BF16, name="sg", tag="sg")
-            if n in SIGN_ON_SCALAR:
-                nc.scalar.activation(out=sg[:], in_=w_sb[n][:], func=ACT.Sign)
-            else:
-                nc.vector.tensor_scalar(
-                    out=sg[:], in0=w_sb[n][:], scalar1=0.0, scalar2=0.5,
-                    op0=ALU.is_ge, op1=ALU.subtract,
-                )
+            nc.vector.tensor_scalar(
+                out=sg[:], in0=w_sb[n][:], scalar1=0.0, scalar2=0.5,
+                op0=ALU.is_ge, op1=ALU.subtract,
+            )
             for a in range(A_T):
                 for g in range(G):
                     j = a * G + g
@@ -164,9 +160,15 @@ def tile_bitlinear_kernel(tc, x, weight, bias, out):
                         stop=(c == C - 1),
                     )
                 o_sb = outp.tile([P, NB], F32, name="o_sb", tag="o_sb")
-                nc.vector.tensor_tensor(
-                    out=o_sb[:], in0=acc[:], in1=bias_bc[:, n * NB : (n + 1) * NB], op=ALU.add
-                )
+                if m in BIAS_ON_GPSIMD:
+                    nc.scalar.copy(out=o_sb[:], in_=acc[:])
+                    nc.gpsimd.tensor_tensor(
+                        out=o_sb[:], in0=o_sb[:], in1=bias_bc[:, n * NB : (n + 1) * NB], op=ALU.add
+                    )
+                else:
+                    nc.vector.tensor_tensor(
+                        out=o_sb[:], in0=acc[:], in1=bias_bc[:, n * NB : (n + 1) * NB], op=ALU.add
+                    )
                 nc.sync.dma_start(
                     out=of[m * P : (m + 1) * P, n * NB : (n + 1) * NB], in_=o_sb[:]
                 )
@@ -179,7 +181,7 @@ def tile_bitlinear_kernel(tc, x, weight, bias, out):
                 for c in range(C):
                     for u in range(2):
                         nc.tensor.transpose(ps[:, c, u, :], xw[:, m, c, u, :], ident_f[:])
-                nc.scalar.copy(
+                nc.vector.tensor_copy(
                     out=xg32[:, :, m * P : (m + 1) * P, :],
                     in_=ps[:].rearrange("p c u k -> p c k u"),
                 )

@@ -23,7 +23,6 @@ A_T = NB // P
 G = K // GROUP
 MT = TOK // P
 C = K // 512
-BIAS_ON_GPSIMD = (7,)
 
 FLOPS = 2 * TOK * K * OUT
 
@@ -52,9 +51,13 @@ def tile_bitlinear_kernel(tc, x, weight, bias, out):
             )
             w_sb.append(w_n)
 
-        load_w(0)
         x_sb = const.tile([P, MT, K], BF16, name="x_sb")
-        nc.sync.dma_start(out=x_sb[:], in_=xf.rearrange("(m p) k -> p m k", p=P))
+        x_view = xf.rearrange("(m p) k -> p m k", p=P)
+        w_0 = wpool.tile([P, A_T, K], BF16, name="w_n", tag="w_n")
+        w_sb.append(w_0)
+        for a in range(A_T):
+            nc.sync.dma_start(out=w_0[:, a, :], in_=weight[a * P : (a + 1) * P, :])
+            nc.sync.dma_start(out=x_sb[:, 2 * a : 2 * a + 2, :], in_=x_view[:, 2 * a : 2 * a + 2, :])
         load_w(1)
         bias_bc = const.tile([P, OUT], BF16, name="bias_bc")
         nc.sync.dma_start(out=bias_bc[:], in_=bias.partition_broadcast(P))
@@ -82,6 +85,7 @@ def tile_bitlinear_kernel(tc, x, weight, bias, out):
                         out=absw[:, a, g * GROUP : (g + 1) * GROUP],
                         in_=w_sb[n][:, a, g * GROUP : (g + 1) * GROUP],
                         func=ACT.Abs,
+                        scale=4.0,
                         accum_out=sums[:, j : j + 1],
                     )
             state[("sums", n)] = sums
@@ -90,27 +94,28 @@ def tile_bitlinear_kernel(tc, x, weight, bias, out):
         def stage_ternary(n):
             sums = state[("sums", n)]
             absw = state[("absw", n)]
-            thr = small.tile([P, A_T * G], F32, name="thr", tag="thr")
             s2 = small.tile([P, A_T * G], F32, name="s2", tag="s2")
-            nc.vector.tensor_scalar(
-                out=thr[:], in0=sums[:], scalar1=1.0 / 256.0, scalar2=EPS / 2.0,
-                op0=ALU.mult, op1=ALU.max,
-            )
-            nc.vector.tensor_scalar(
-                out=s2[:], in0=sums[:], scalar1=1.0 / 64.0, scalar2=EPS * 2.0,
-                op0=ALU.mult, op1=ALU.max,
-            )
             sg = work.tile([P, A_T, K], BF16, name="sg", tag="sg")
-            nc.vector.tensor_scalar(
-                out=sg[:], in0=w_sb[n][:], scalar1=0.0, scalar2=0.5,
-                op0=ALU.is_ge, op1=ALU.subtract,
-            )
+            pieces = A_T if n == 0 else 1
+            step = A_T // pieces
+            for q in range(pieces):
+                nc.vector.tensor_scalar(
+                    out=sg[:, q * step : (q + 1) * step, :],
+                    in0=w_sb[n][:, q * step : (q + 1) * step, :],
+                    scalar1=0.0, scalar2=0.5, op0=ALU.is_ge, op1=ALU.subtract,
+                )
+            for q in range(pieces):
+                nc.vector.tensor_scalar(
+                    out=s2[:, q * step * G : (q + 1) * step * G],
+                    in0=sums[:, q * step * G : (q + 1) * step * G],
+                    scalar1=1.0 / 256.0, scalar2=EPS * 2.0, op0=ALU.mult, op1=ALU.max,
+                )
             for a in range(A_T):
                 for g in range(G):
                     j = a * G + g
                     sl = absw[:, a, g * GROUP : (g + 1) * GROUP]
                     nc.vector.tensor_scalar(
-                        out=sl, in0=sl, scalar1=thr[:, j : j + 1], scalar2=s2[:, j : j + 1],
+                        out=sl, in0=sl, scalar1=s2[:, j : j + 1], scalar2=s2[:, j : j + 1],
                         op0=ALU.is_gt, op1=ALU.mult,
                     )
                 nc.vector.tensor_tensor(
@@ -160,15 +165,9 @@ def tile_bitlinear_kernel(tc, x, weight, bias, out):
                         stop=(c == C - 1),
                     )
                 o_sb = outp.tile([P, NB], F32, name="o_sb", tag="o_sb")
-                if m in BIAS_ON_GPSIMD:
-                    nc.scalar.copy(out=o_sb[:], in_=acc[:])
-                    nc.gpsimd.tensor_tensor(
-                        out=o_sb[:], in0=o_sb[:], in1=bias_bc[:, n * NB : (n + 1) * NB], op=ALU.add
-                    )
-                else:
-                    nc.vector.tensor_tensor(
-                        out=o_sb[:], in0=acc[:], in1=bias_bc[:, n * NB : (n + 1) * NB], op=ALU.add
-                    )
+                nc.vector.tensor_tensor(
+                    out=o_sb[:], in0=acc[:], in1=bias_bc[:, n * NB : (n + 1) * NB], op=ALU.add
+                )
                 nc.sync.dma_start(
                     out=of[m * P : (m + 1) * P, n * NB : (n + 1) * NB], in_=o_sb[:]
                 )

@@ -23,6 +23,10 @@ A_T = NB // P
 G = K // GROUP
 MT = TOK // P
 C = K // 512
+FOLD_OF = [0, 3, 3, 3, 3, 3, 3, 3]
+NN = 16
+XCOPY_ON_SCALAR = ()
+SIGN_ON_SCALAR = (1, 3, 5, 7)
 
 FLOPS = 2 * TOK * K * OUT
 
@@ -39,7 +43,8 @@ def tile_bitlinear_kernel(tc, x, weight, bias, out):
         codes = ctx.enter_context(tc.tile_pool(name="codes", bufs=3))
         outp = ctx.enter_context(tc.tile_pool(name="outp", bufs=6))
         psum_t = ctx.enter_context(tc.psum_pool(name="psum_t", bufs=3))
-        psum_a = ctx.enter_context(tc.psum_pool(name="psum_a", bufs=4))
+        psum_a = ctx.enter_context(tc.psum_pool(name="psum_a", bufs=3))
+        psum_f = ctx.enter_context(tc.psum_pool(name="psum_f", bufs=2))
 
         w_sb = []
 
@@ -75,19 +80,43 @@ def tile_bitlinear_kernel(tc, x, weight, bias, out):
 
         state = {}
 
+        def gain(n):
+            return 2.0 if n in SIGN_ON_SCALAR else 4.0
+
         def stage_sums(n):
             sums = small.tile([P, A_T * G], F32, name="sums", tag="sums")
             absw = work.tile([P, A_T, K], BF16, name="absw", tag="absw")
-            for a in range(A_T):
+            fold = FOLD_OF[n]
+            if fold:
+                ps_f = psum_f.tile([P, fold, G, NN], F32, name="ps_f", tag="ps_f")
+            for a in range(fold):
+                nc.scalar.activation(out=absw[:, a, :], in_=w_sb[n][:, a, :], func=ACT.Abs, scale=gain(n))
+                view = absw[:, a, :].rearrange("p (g i n) -> p i g n", g=G, n=NN)
+                for i in range(GROUP // NN):
+                    nc.tensor.matmul(
+                        out=ps_f[:, a, :, :],
+                        lhsT=ident_b[:],
+                        rhs=view[:, i, :, :],
+                        start=(i == 0),
+                        stop=(i == GROUP // NN - 1),
+                    )
+            for a in range(fold, A_T):
                 for g in range(G):
                     j = a * G + g
                     nc.scalar.activation(
                         out=absw[:, a, g * GROUP : (g + 1) * GROUP],
                         in_=w_sb[n][:, a, g * GROUP : (g + 1) * GROUP],
                         func=ACT.Abs,
-                        scale=4.0,
+                        scale=gain(n),
                         accum_out=sums[:, j : j + 1],
                     )
+            if fold:
+                nc.vector.tensor_reduce(
+                    out=sums[:, 0 : fold * G],
+                    in_=ps_f[:].rearrange("p a g n -> p (a g) n"),
+                    axis=mybir.AxisListType.X,
+                    op=ALU.add,
+                )
             state[("sums", n)] = sums
             state[("absw", n)] = absw
 
@@ -98,7 +127,10 @@ def tile_bitlinear_kernel(tc, x, weight, bias, out):
             sg = work.tile([P, A_T, K], BF16, name="sg", tag="sg")
             pieces = A_T if n == 0 else 1
             step = A_T // pieces
-            for q in range(pieces):
+            if n in SIGN_ON_SCALAR:
+                for a in range(A_T):
+                    nc.scalar.activation(out=sg[:, a, :], in_=w_sb[n][:, a, :], func=ACT.Sign)
+            for q in range(pieces if n not in SIGN_ON_SCALAR else 0):
                 nc.vector.tensor_scalar(
                     out=sg[:, q * step : (q + 1) * step, :],
                     in0=w_sb[n][:, q * step : (q + 1) * step, :],
@@ -108,7 +140,7 @@ def tile_bitlinear_kernel(tc, x, weight, bias, out):
                 nc.vector.tensor_scalar(
                     out=s2[:, q * step * G : (q + 1) * step * G],
                     in0=sums[:, q * step * G : (q + 1) * step * G],
-                    scalar1=1.0 / 256.0, scalar2=EPS * 2.0, op0=ALU.mult, op1=ALU.max,
+                    scalar1=1.0 / 256.0, scalar2=EPS * gain(n) / 2.0, op0=ALU.mult, op1=ALU.max,
                 )
             for a in range(A_T):
                 for g in range(G):
@@ -180,10 +212,16 @@ def tile_bitlinear_kernel(tc, x, weight, bias, out):
                 for c in range(C):
                     for u in range(2):
                         nc.tensor.transpose(ps[:, c, u, :], xw[:, m, c, u, :], ident_f[:])
-                nc.vector.tensor_copy(
-                    out=xg32[:, :, m * P : (m + 1) * P, :],
-                    in_=ps[:].rearrange("p c u k -> p c k u"),
-                )
+                if m in XCOPY_ON_SCALAR:
+                    nc.scalar.copy(
+                        out=xg32[:, :, m * P : (m + 1) * P, :],
+                        in_=ps[:].rearrange("p c u k -> p c k u"),
+                    )
+                else:
+                    nc.vector.tensor_copy(
+                        out=xg32[:, :, m * P : (m + 1) * P, :],
+                        in_=ps[:].rearrange("p c u k -> p c k u"),
+                    )
             for c in range(C):
                 for h in range(2):
                     sl = slice(h * 512, (h + 1) * 512)

@@ -23,10 +23,6 @@ A_T = NB // P
 G = K // GROUP
 MT = TOK // P
 C = K // 512
-FOLD_OF = [0, 3, 3, 3, 3, 3, 3, 3]
-NN = 16
-XCOPY_ON_SCALAR = ()
-SIGN_ON_SCALAR = (1, 3, 5, 7)
 
 FLOPS = 2 * TOK * K * OUT
 
@@ -41,10 +37,9 @@ def tile_bitlinear_kernel(tc, x, weight, bias, out):
         work = ctx.enter_context(tc.tile_pool(name="work", bufs=2))
         small = ctx.enter_context(tc.tile_pool(name="small", bufs=3))
         codes = ctx.enter_context(tc.tile_pool(name="codes", bufs=3))
-        outp = ctx.enter_context(tc.tile_pool(name="outp", bufs=6))
+        outp = ctx.enter_context(tc.tile_pool(name="outp", bufs=8))
         psum_t = ctx.enter_context(tc.psum_pool(name="psum_t", bufs=3))
-        psum_a = ctx.enter_context(tc.psum_pool(name="psum_a", bufs=3))
-        psum_f = ctx.enter_context(tc.psum_pool(name="psum_f", bufs=2))
+        psum_a = ctx.enter_context(tc.psum_pool(name="psum_a", bufs=5))
 
         w_sb = []
 
@@ -80,43 +75,19 @@ def tile_bitlinear_kernel(tc, x, weight, bias, out):
 
         state = {}
 
-        def gain(n):
-            return 2.0 if n in SIGN_ON_SCALAR else 4.0
-
         def stage_sums(n):
             sums = small.tile([P, A_T * G], F32, name="sums", tag="sums")
             absw = work.tile([P, A_T, K], BF16, name="absw", tag="absw")
-            fold = FOLD_OF[n]
-            if fold:
-                ps_f = psum_f.tile([P, fold, G, NN], F32, name="ps_f", tag="ps_f")
-            for a in range(fold):
-                nc.scalar.activation(out=absw[:, a, :], in_=w_sb[n][:, a, :], func=ACT.Abs, scale=gain(n))
-                view = absw[:, a, :].rearrange("p (g i n) -> p i g n", g=G, n=NN)
-                for i in range(GROUP // NN):
-                    nc.tensor.matmul(
-                        out=ps_f[:, a, :, :],
-                        lhsT=ident_b[:],
-                        rhs=view[:, i, :, :],
-                        start=(i == 0),
-                        stop=(i == GROUP // NN - 1),
-                    )
-            for a in range(fold, A_T):
+            for a in range(A_T):
                 for g in range(G):
                     j = a * G + g
                     nc.scalar.activation(
                         out=absw[:, a, g * GROUP : (g + 1) * GROUP],
                         in_=w_sb[n][:, a, g * GROUP : (g + 1) * GROUP],
                         func=ACT.Abs,
-                        scale=gain(n),
+                        scale=4.0,
                         accum_out=sums[:, j : j + 1],
                     )
-            if fold:
-                nc.vector.tensor_reduce(
-                    out=sums[:, 0 : fold * G],
-                    in_=ps_f[:].rearrange("p a g n -> p (a g) n"),
-                    axis=mybir.AxisListType.X,
-                    op=ALU.add,
-                )
             state[("sums", n)] = sums
             state[("absw", n)] = absw
 
@@ -127,10 +98,7 @@ def tile_bitlinear_kernel(tc, x, weight, bias, out):
             sg = work.tile([P, A_T, K], BF16, name="sg", tag="sg")
             pieces = A_T if n == 0 else 1
             step = A_T // pieces
-            if n in SIGN_ON_SCALAR:
-                for a in range(A_T):
-                    nc.scalar.activation(out=sg[:, a, :], in_=w_sb[n][:, a, :], func=ACT.Sign)
-            for q in range(pieces if n not in SIGN_ON_SCALAR else 0):
+            for q in range(pieces):
                 nc.vector.tensor_scalar(
                     out=sg[:, q * step : (q + 1) * step, :],
                     in0=w_sb[n][:, q * step : (q + 1) * step, :],
@@ -140,7 +108,7 @@ def tile_bitlinear_kernel(tc, x, weight, bias, out):
                 nc.vector.tensor_scalar(
                     out=s2[:, q * step * G : (q + 1) * step * G],
                     in0=sums[:, q * step * G : (q + 1) * step * G],
-                    scalar1=1.0 / 256.0, scalar2=EPS * gain(n) / 2.0, op0=ALU.mult, op1=ALU.max,
+                    scalar1=1.0 / 256.0, scalar2=EPS * 2.0, op0=ALU.mult, op1=ALU.max,
                 )
             for a in range(A_T):
                 for g in range(G):
@@ -212,16 +180,10 @@ def tile_bitlinear_kernel(tc, x, weight, bias, out):
                 for c in range(C):
                     for u in range(2):
                         nc.tensor.transpose(ps[:, c, u, :], xw[:, m, c, u, :], ident_f[:])
-                if m in XCOPY_ON_SCALAR:
-                    nc.scalar.copy(
-                        out=xg32[:, :, m * P : (m + 1) * P, :],
-                        in_=ps[:].rearrange("p c u k -> p c k u"),
-                    )
-                else:
-                    nc.vector.tensor_copy(
-                        out=xg32[:, :, m * P : (m + 1) * P, :],
-                        in_=ps[:].rearrange("p c u k -> p c k u"),
-                    )
+                nc.vector.tensor_copy(
+                    out=xg32[:, :, m * P : (m + 1) * P, :],
+                    in_=ps[:].rearrange("p c u k -> p c k u"),
+                )
             for c in range(C):
                 for h in range(2):
                     sl = slice(h * 512, (h + 1) * 512)

@@ -66,8 +66,6 @@ def tile_bitlinear_kernel(tc, x, weight, bias, out):
 
         ident_f = const.tile([P, P], F32, name="ident_f")
         make_identity(nc, ident_f[:])
-        ident_b = const.tile([P, P], BF16, name="ident_b")
-        make_identity(nc, ident_b[:])
 
         xg = const.tile([P, C, TOK, 4], BF16, name="xg", align_bytes=64)
         x_codes = const.tile([P, C, TOK], U32, name="x_codes", align_bytes=64)
@@ -126,15 +124,16 @@ def tile_bitlinear_kernel(tc, x, weight, bias, out):
         def stage_transpose(n):
             wq = state[("wq", n)]
             grouped = work.tile([P, C, NB, 4], BF16, name="grouped", tag="grouped", align_bytes=64)
+            words = wq[:].bitcast(F32).rearrange("p a (c q u) -> p a c u q", c=C, u=2)
+            grouped32 = grouped[:].bitcast(F32)
             for a in range(A_T):
-                ps = psum_t.tile([P, C, 4, P], BF16, name="ps_w", tag="tp")
-                view = wq[:, a, :].rearrange("p (c q t) -> p c t q", c=C, t=4)
+                ps = psum_t.tile([P, C, 2, P], F32, name="ps_w", tag="tp")
                 for c in range(C):
-                    for t in range(4):
-                        nc.tensor.transpose(ps[:, c, t, :], view[:, c, t, :], ident_b[:])
+                    for u in range(2):
+                        nc.tensor.transpose(ps[:, c, u, :], words[:, a, c, u, :], ident_f[:])
                 nc.scalar.copy(
-                    out=grouped[:, :, a * P : (a + 1) * P, :],
-                    in_=ps[:].rearrange("p c t o -> p c o t"),
+                    out=grouped32[:, :, a * P : (a + 1) * P, :],
+                    in_=ps[:].rearrange("p c u o -> p c o u"),
                 )
             state[("grouped", n)] = grouped
 

@@ -23,6 +23,9 @@ A_T = NB // P
 G = K // GROUP
 MT = TOK // P
 C = K // 512
+LEAD = 3
+TURN_BANKS = 3
+ACC_BANKS = 5
 
 FLOPS = 2 * TOK * K * OUT
 
@@ -35,11 +38,12 @@ def tile_bitlinear_kernel(tc, x, weight, bias, out):
         const = ctx.enter_context(tc.tile_pool(name="const", bufs=1))
         wpool = ctx.enter_context(tc.tile_pool(name="wpool", bufs=NBLK))
         work = ctx.enter_context(tc.tile_pool(name="work", bufs=2))
-        small = ctx.enter_context(tc.tile_pool(name="small", bufs=3))
+        small = ctx.enter_context(tc.tile_pool(name="small", bufs=4))
         codes = ctx.enter_context(tc.tile_pool(name="codes", bufs=3))
         outp = ctx.enter_context(tc.tile_pool(name="outp", bufs=8))
-        psum_t = ctx.enter_context(tc.psum_pool(name="psum_t", bufs=3))
-        psum_a = ctx.enter_context(tc.psum_pool(name="psum_a", bufs=5))
+        psum_t = ctx.enter_context(tc.psum_pool(name="psum_t", bufs=TURN_BANKS))
+        psum_a = ctx.enter_context(tc.psum_pool(name="psum_a", bufs=ACC_BANKS))
+        ctx.enter_context(tc.manual_schedule())
 
         w_sb = []
 
@@ -71,139 +75,151 @@ def tile_bitlinear_kernel(tc, x, weight, bias, out):
         x_codes = const.tile([P, C, TOK], U32, name="x_codes", align_bytes=64)
         x_scales = const.tile([P, C, TOK], U8, name="x_scales", align_bytes=64)
 
-        state = {}
+        sums, absw, scales2, sg, grouped, w_codes, w_scales, acc = {}, {}, {}, {}, {}, {}, {}, {}
+        bank = {}
+        xw = x_sb[:].bitcast(F32).rearrange("p m (c q u) -> p m c u q", c=C, u=2)
+        xg32 = xg[:].bitcast(F32)
 
-        def stage_sums(n):
-            sums = small.tile([P, A_T * G], F32, name="sums", tag="sums")
-            absw = work.tile([P, A_T, K], BF16, name="absw", tag="absw")
-            for a in range(A_T):
-                for g in range(G):
-                    j = a * G + g
-                    nc.scalar.activation(
-                        out=absw[:, a, g * GROUP : (g + 1) * GROUP],
-                        in_=w_sb[n][:, a, g * GROUP : (g + 1) * GROUP],
-                        func=ACT.Abs,
-                        scale=4.0,
-                        accum_out=sums[:, j : j + 1],
-                    )
-            state[("sums", n)] = sums
-            state[("absw", n)] = absw
+        def S_sum(n, a):
+            if a == 0:
+                sums[n] = small.tile([P, A_T * G], F32, name="sums", tag="sums")
+                absw[n] = work.tile([P, A_T, K], BF16, name="absw", tag="absw", bufs=3)
+                scales2[n] = small.tile([P, A_T * G], F32, name="s2", tag="s2")
+            for g in range(G):
+                j = a * G + g
+                nc.scalar.activation(
+                    out=absw[n][:, a, g * GROUP : (g + 1) * GROUP],
+                    in_=w_sb[n][:, a, g * GROUP : (g + 1) * GROUP],
+                    func=ACT.Abs,
+                    scale=4.0,
+                    accum_out=sums[n][:, j : j + 1],
+                )
 
-        def stage_ternary(n):
-            sums = state[("sums", n)]
-            absw = state[("absw", n)]
-            s2 = small.tile([P, A_T * G], F32, name="s2", tag="s2")
-            sg = work.tile([P, A_T, K], BF16, name="sg", tag="sg")
-            pieces = A_T if n == 0 else 1
-            step = A_T // pieces
-            for q in range(pieces):
+        def sign(n, a=None):
+            if a is None or a == 0:
+                sg[n] = work.tile([P, A_T, K], BF16, name="sg", tag="sg", bufs=3)
+            sl = slice(0, A_T) if a is None else slice(a, a + 1)
+            nc.vector.tensor_scalar(
+                out=sg[n][:, sl, :], in0=w_sb[n][:, sl, :],
+                scalar1=0.0, scalar2=0.5, op0=ALU.is_ge, op1=ALU.subtract,
+            )
+
+        def s2(n, a0, a1):
+            nc.vector.tensor_scalar(
+                out=scales2[n][:, a0 * G : a1 * G], in0=sums[n][:, a0 * G : a1 * G],
+                scalar1=1.0 / 256.0, scalar2=EPS * 2.0, op0=ALU.mult, op1=ALU.max,
+            )
+
+        def masks(n, a):
+            for g in range(G):
+                j = a * G + g
+                sl = absw[n][:, a, g * GROUP : (g + 1) * GROUP]
                 nc.vector.tensor_scalar(
-                    out=sg[:, q * step : (q + 1) * step, :],
-                    in0=w_sb[n][:, q * step : (q + 1) * step, :],
-                    scalar1=0.0, scalar2=0.5, op0=ALU.is_ge, op1=ALU.subtract,
+                    out=sl, in0=sl, scalar1=scales2[n][:, j : j + 1], scalar2=scales2[n][:, j : j + 1],
+                    op0=ALU.is_gt, op1=ALU.mult,
                 )
-            for q in range(pieces):
-                nc.vector.tensor_scalar(
-                    out=s2[:, q * step * G : (q + 1) * step * G],
-                    in0=sums[:, q * step * G : (q + 1) * step * G],
-                    scalar1=1.0 / 256.0, scalar2=EPS * 2.0, op0=ALU.mult, op1=ALU.max,
-                )
-            for a in range(A_T):
-                for g in range(G):
-                    j = a * G + g
-                    sl = absw[:, a, g * GROUP : (g + 1) * GROUP]
-                    nc.vector.tensor_scalar(
-                        out=sl, in0=sl, scalar1=s2[:, j : j + 1], scalar2=s2[:, j : j + 1],
-                        op0=ALU.is_gt, op1=ALU.mult,
-                    )
-                nc.vector.tensor_tensor(
-                    out=sg[:, a, :], in0=absw[:, a, :], in1=sg[:, a, :], op=ALU.mult
-                )
-            state[("wq", n)] = sg
 
-        def stage_transpose(n):
-            wq = state[("wq", n)]
-            grouped = work.tile([P, C, NB, 4], BF16, name="grouped", tag="grouped", align_bytes=64)
-            words = wq[:].bitcast(F32).rearrange("p a (c q u) -> p a c u q", c=C, u=2)
-            grouped32 = grouped[:].bitcast(F32)
-            for a in range(A_T):
-                ps = psum_t.tile([P, C, 2, P], F32, name="ps_w", tag="tp")
-                for c in range(C):
-                    for u in range(2):
-                        nc.tensor.transpose(ps[:, c, u, :], words[:, a, c, u, :], ident_f[:])
-                nc.scalar.copy(
-                    out=grouped32[:, :, a * P : (a + 1) * P, :],
-                    in_=ps[:].rearrange("p c u o -> p c o u"),
-                )
-            state[("grouped", n)] = grouped
+        def prod(n, a):
+            nc.vector.tensor_tensor(
+                out=sg[n][:, a, :], in0=absw[n][:, a, :], in1=sg[n][:, a, :], op=ALU.mult
+            )
 
-        def stage_quant(n):
-            grouped = state[("grouped", n)]
-            w_codes = codes.tile([P, C, NB], U32, name="w_codes", tag="w_codes", align_bytes=64)
-            w_scales = codes.tile([P, C, NB], U8, name="w_scales", tag="w_scales", align_bytes=64)
+        def T(n, a):
+            words = sg[n][:].bitcast(F32).rearrange("p a (c q u) -> p a c u q", c=C, u=2)
+            bank["w", n, a] = psum_t.tile([P, C, 2, P], F32, name="ps_w", tag="tp")
+            for c in range(C):
+                for u in range(2):
+                    nc.tensor.transpose(bank["w", n, a][:, c, u, :], words[:, a, c, u, :], ident_f[:])
+
+        def E(n, a):
+            if a == 0:
+                grouped[n] = work.tile([P, C, NB, 4], BF16, name="grouped", tag="grouped", align_bytes=64)
+            nc.scalar.copy(
+                out=grouped[n][:].bitcast(F32)[:, :, a * P : (a + 1) * P, :],
+                in_=bank["w", n, a][:].rearrange("p c u o -> p c o u"),
+            )
+
+        def q(n, c0, c1):
+            if c0 == 0:
+                w_codes[n] = codes.tile([P, C, NB], U32, name="w_codes", tag="w_codes", align_bytes=64)
+                w_scales[n] = codes.tile([P, C, NB], U8, name="w_scales", tag="w_scales", align_bytes=64)
+            for c in range(c0, c1):
+                nc.vector.quantize_mx(
+                    out=w_codes[n][:, c, :].bitcast(FP8X4),
+                    scales=w_scales[n][:, c, :],
+                    in_=grouped[n][:, c, :, :].rearrange("p o t -> p (o t)"),
+                )
+
+        def MX(n, m):
+            acc[n, m] = psum_a.tile([P, NB], F32, name="acc", tag="acc")
+            for c in range(C):
+                nc.tensor.matmul_mx(
+                    out=acc[n, m][:],
+                    lhsT=x_codes[:, c, m * P : (m + 1) * P].bitcast(FP8X4),
+                    lhsT_scale=x_scales[:, c, m * P : (m + 1) * P],
+                    rhs=w_codes[n][:, c, :].bitcast(FP8X4),
+                    rhs_scale=w_scales[n][:, c, :],
+                    start=(c == 0),
+                    stop=(c == C - 1),
+                )
+
+        def ev(n, m):
+            o_sb = outp.tile([P, NB], F32, name="o_sb", tag="o_sb")
+            nc.vector.tensor_tensor(
+                out=o_sb[:], in0=acc[n, m][:], in1=bias_bc[:, n * NB : (n + 1) * NB], op=ALU.add
+            )
+            nc.sync.dma_start(out=of[m * P : (m + 1) * P, n * NB : (n + 1) * NB], in_=o_sb[:])
+
+        def xT(m):
+            bank["x", m] = psum_t.tile([P, C, 2, P], F32, name="ps_x", tag="tp")
+            for c in range(C):
+                for u in range(2):
+                    nc.tensor.transpose(bank["x", m][:, c, u, :], xw[:, m, c, u, :], ident_f[:])
+
+        def xc(m):
+            nc.vector.tensor_copy(
+                out=xg32[:, :, m * P : (m + 1) * P, :],
+                in_=bank["x", m][:].rearrange("p c u k -> p c k u"),
+            )
+
+        def qx(h):
+            sl = slice(h * 512, (h + 1) * 512)
             for c in range(C):
                 nc.vector.quantize_mx(
-                    out=w_codes[:, c, :].bitcast(FP8X4),
-                    scales=w_scales[:, c, :],
-                    in_=grouped[:, c, :, :].rearrange("p o t -> p (o t)"),
-                )
-            state[("codes", n)] = (w_codes, w_scales)
-
-        def stage_mm(n):
-            w_codes, w_scales = state[("codes", n)]
-            for m in range(MT):
-                acc = psum_a.tile([P, NB], F32, name="acc", tag="acc")
-                for c in range(C):
-                    nc.tensor.matmul_mx(
-                        out=acc[:],
-                        lhsT=x_codes[:, c, m * P : (m + 1) * P].bitcast(FP8X4),
-                        lhsT_scale=x_scales[:, c, m * P : (m + 1) * P],
-                        rhs=w_codes[:, c, :].bitcast(FP8X4),
-                        rhs_scale=w_scales[:, c, :],
-                        start=(c == 0),
-                        stop=(c == C - 1),
-                    )
-                o_sb = outp.tile([P, NB], F32, name="o_sb", tag="o_sb")
-                nc.vector.tensor_tensor(
-                    out=o_sb[:], in0=acc[:], in1=bias_bc[:, n * NB : (n + 1) * NB], op=ALU.add
-                )
-                nc.sync.dma_start(
-                    out=of[m * P : (m + 1) * P, n * NB : (n + 1) * NB], in_=o_sb[:]
+                    out=x_codes[:, c, sl].bitcast(FP8X4),
+                    scales=x_scales[:, c, sl],
+                    in_=xg[:, c, sl, :].rearrange("p k t -> p (k t)"),
                 )
 
-        def stage_x():
-            xw = x_sb[:].bitcast(F32).rearrange("p m (c q u) -> p m c u q", c=C, u=2)
-            xg32 = xg[:].bitcast(F32)
-            for m in range(MT):
-                ps = psum_t.tile([P, C, 2, P], F32, name="ps_x", tag="tp")
-                for c in range(C):
-                    for u in range(2):
-                        nc.tensor.transpose(ps[:, c, u, :], xw[:, m, c, u, :], ident_f[:])
-                nc.vector.tensor_copy(
-                    out=xg32[:, :, m * P : (m + 1) * P, :],
-                    in_=ps[:].rearrange("p c u k -> p c k u"),
-                )
-            for c in range(C):
-                for h in range(2):
-                    sl = slice(h * 512, (h + 1) * 512)
-                    nc.vector.quantize_mx(
-                        out=x_codes[:, c, sl].bitcast(FP8X4),
-                        scales=x_scales[:, c, sl],
-                        in_=xg[:, c, sl, :].rearrange("p k t -> p (k t)"),
-                    )
-
-        stage_sums(0)
-        stage_x()
-        stage_ternary(0)
-        stage_sums(1)
-        stage_transpose(0)
-        stage_quant(0)
-        for n in range(NBLK):
-            if n + 1 < NBLK:
-                stage_ternary(n + 1)
-            if n + 2 < NBLK:
-                stage_sums(n + 2)
-            stage_mm(n)
-            if n + 1 < NBLK:
-                stage_transpose(n + 1)
-                stage_quant(n + 1)
+        for t in range(-28, NBLK * MT):
+            for b in range(NBLK):
+                d = t - MT * b
+                if -28 <= d <= -22 and d % 2 == 0:
+                    S_sum(b, (d + 28) // 2)
+                if d in (-11, -9):
+                    for a in (0, 1) if d == -11 else (2, 3):
+                        T(b, a)
+                        E(b, a)
+            if -20 <= t <= -17:
+                for m in (2 * (t + 20), 2 * (t + 20) + 1):
+                    xT(m)
+                    xc(m)
+            j = t + LEAD
+            if 0 <= j < NBLK * MT:
+                MX(j // MT, j % MT)
+            if t >= 0:
+                ev(t // MT, t % MT)
+            if t in (-14, -13):
+                qx(t + 14)
+            for b in range(NBLK):
+                d = t - MT * b
+                if -18 <= d <= -15:
+                    masks(b, d + 18)
+                if -14 <= d <= -11:
+                    prod(b, d + 14)
+                if d in (-6, -5):
+                    q(b, d + 6, d + 7)
+                if -20 <= d <= -17:
+                    sign(b, d + 20)
+                if d == -19:
+                    s2(b, 0, A_T)

@@ -23,9 +23,18 @@ A_T = NB // P
 G = K // GROUP
 MT = TOK // P
 C = K // 512
+SIGN_SCALAR = (6, 7)
+
+SUMS = -29
+SIGNS = -20
+MASKS = -20
+PRODUCTS = -15
+TURNS = -14
+COPIES = -8
+QUANTISE = -4
 LEAD = 3
-TURN_BANKS = 3
-ACC_BANKS = 5
+HEAD = -29
+HEAD_COPIES = 20
 
 FLOPS = 2 * TOK * K * OUT
 
@@ -37,12 +46,12 @@ def tile_bitlinear_kernel(tc, x, weight, bias, out):
     with ExitStack() as ctx:
         const = ctx.enter_context(tc.tile_pool(name="const", bufs=1))
         wpool = ctx.enter_context(tc.tile_pool(name="wpool", bufs=NBLK))
-        work = ctx.enter_context(tc.tile_pool(name="work", bufs=2))
+        work = ctx.enter_context(tc.tile_pool(name="work", bufs=3))
         small = ctx.enter_context(tc.tile_pool(name="small", bufs=4))
         codes = ctx.enter_context(tc.tile_pool(name="codes", bufs=3))
         outp = ctx.enter_context(tc.tile_pool(name="outp", bufs=8))
-        psum_t = ctx.enter_context(tc.psum_pool(name="psum_t", bufs=TURN_BANKS))
-        psum_a = ctx.enter_context(tc.psum_pool(name="psum_a", bufs=ACC_BANKS))
+        psum_t = ctx.enter_context(tc.psum_pool(name="psum_t", bufs=4))
+        psum_a = ctx.enter_context(tc.psum_pool(name="psum_a", bufs=4))
         ctx.enter_context(tc.manual_schedule())
 
         w_sb = []
@@ -59,13 +68,16 @@ def tile_bitlinear_kernel(tc, x, weight, bias, out):
         x_view = xf.rearrange("(m p) k -> p m k", p=P)
         w_0 = wpool.tile([P, A_T, K], BF16, name="w_n", tag="w_n")
         w_sb.append(w_0)
-        for a in range(A_T):
-            nc.sync.dma_start(out=w_0[:, a, :], in_=weight[a * P : (a + 1) * P, :])
-            nc.sync.dma_start(out=x_sb[:, 2 * a : 2 * a + 2, :], in_=x_view[:, 2 * a : 2 * a + 2, :])
+        for m in range(A_T):
+            nc.sync.dma_start(out=w_0[:, m, :], in_=weight[m * P : (m + 1) * P, :])
+            nc.sync.dma_start(out=x_sb[:, m, :], in_=x_view[:, m, :])
         load_w(1)
+        for m in range(A_T, MT):
+            nc.sync.dma_start(out=x_sb[:, m, :], in_=x_view[:, m, :])
+        load_w(2)
         bias_bc = const.tile([P, OUT], BF16, name="bias_bc")
         nc.sync.dma_start(out=bias_bc[:], in_=bias.partition_broadcast(P))
-        for n in range(2, NBLK):
+        for n in range(3, NBLK):
             load_w(n)
 
         ident_f = const.tile([P, P], F32, name="ident_f")
@@ -75,15 +87,20 @@ def tile_bitlinear_kernel(tc, x, weight, bias, out):
         x_codes = const.tile([P, C, TOK], U32, name="x_codes", align_bytes=64)
         x_scales = const.tile([P, C, TOK], U8, name="x_scales", align_bytes=64)
 
-        sums, absw, scales2, sg, grouped, w_codes, w_scales, acc = {}, {}, {}, {}, {}, {}, {}, {}
-        bank = {}
+        sums, absw, scales2, sg, grouped, w_codes, w_scales, acc, bank = {}, {}, {}, {}, {}, {}, {}, {}, {}
         xw = x_sb[:].bitcast(F32).rearrange("p m (c q u) -> p m c u q", c=C, u=2)
         xg32 = xg[:].bitcast(F32)
+
+        def sign_scalar(n):
+            return n in SIGN_SCALAR
+
+        def alpha(n):
+            return 2.0 if sign_scalar(n) else 4.0
 
         def S_sum(n, a):
             if a == 0:
                 sums[n] = small.tile([P, A_T * G], F32, name="sums", tag="sums")
-                absw[n] = work.tile([P, A_T, K], BF16, name="absw", tag="absw", bufs=3)
+                absw[n] = work.tile([P, A_T, K], BF16, name="absw", tag="absw")
                 scales2[n] = small.tile([P, A_T * G], F32, name="s2", tag="s2")
             for g in range(G):
                 j = a * G + g
@@ -91,23 +108,25 @@ def tile_bitlinear_kernel(tc, x, weight, bias, out):
                     out=absw[n][:, a, g * GROUP : (g + 1) * GROUP],
                     in_=w_sb[n][:, a, g * GROUP : (g + 1) * GROUP],
                     func=ACT.Abs,
-                    scale=4.0,
+                    scale=alpha(n),
                     accum_out=sums[n][:, j : j + 1],
                 )
 
-        def sign(n, a=None):
-            if a is None or a == 0:
-                sg[n] = work.tile([P, A_T, K], BF16, name="sg", tag="sg", bufs=3)
-            sl = slice(0, A_T) if a is None else slice(a, a + 1)
-            nc.vector.tensor_scalar(
-                out=sg[n][:, sl, :], in0=w_sb[n][:, sl, :],
-                scalar1=0.0, scalar2=0.5, op0=ALU.is_ge, op1=ALU.subtract,
-            )
+        def sign(n, a0, a1):
+            if a0 == 0:
+                sg[n] = work.tile([P, A_T, K], BF16, name="sg", tag="sg")
+            if sign_scalar(n):
+                nc.scalar.activation(out=sg[n][:, a0:a1, :], in_=w_sb[n][:, a0:a1, :], func=ACT.Sign)
+            else:
+                nc.vector.tensor_scalar(
+                    out=sg[n][:, a0:a1, :], in0=w_sb[n][:, a0:a1, :],
+                    scalar1=0.0, scalar2=0.5, op0=ALU.is_ge, op1=ALU.subtract,
+                )
 
         def s2(n, a0, a1):
             nc.vector.tensor_scalar(
                 out=scales2[n][:, a0 * G : a1 * G], in0=sums[n][:, a0 * G : a1 * G],
-                scalar1=1.0 / 256.0, scalar2=EPS * 2.0, op0=ALU.mult, op1=ALU.max,
+                scalar1=1.0 / 256.0, scalar2=EPS * alpha(n) / 2, op0=ALU.mult, op1=ALU.max,
             )
 
         def masks(n, a):
@@ -119,9 +138,10 @@ def tile_bitlinear_kernel(tc, x, weight, bias, out):
                     op0=ALU.is_gt, op1=ALU.mult,
                 )
 
-        def prod(n, a):
+        def prod2(n, a):
             nc.vector.tensor_tensor(
-                out=sg[n][:, a, :], in0=absw[n][:, a, :], in1=sg[n][:, a, :], op=ALU.mult
+                out=sg[n][:, a : a + 2, :], in0=absw[n][:, a : a + 2, :], in1=sg[n][:, a : a + 2, :],
+                op=ALU.mult,
             )
 
         def T(n, a):
@@ -133,22 +153,20 @@ def tile_bitlinear_kernel(tc, x, weight, bias, out):
 
         def E(n, a):
             if a == 0:
-                grouped[n] = work.tile([P, C, NB, 4], BF16, name="grouped", tag="grouped", align_bytes=64)
+                grouped[n] = work.tile([P, C, NB, 4], BF16, name="grouped", tag="grouped", bufs=2, align_bytes=64)
             nc.scalar.copy(
                 out=grouped[n][:].bitcast(F32)[:, :, a * P : (a + 1) * P, :],
                 in_=bank["w", n, a][:].rearrange("p c u o -> p c o u"),
             )
 
-        def q(n, c0, c1):
-            if c0 == 0:
-                w_codes[n] = codes.tile([P, C, NB], U32, name="w_codes", tag="w_codes", align_bytes=64)
-                w_scales[n] = codes.tile([P, C, NB], U8, name="w_scales", tag="w_scales", align_bytes=64)
-            for c in range(c0, c1):
-                nc.vector.quantize_mx(
-                    out=w_codes[n][:, c, :].bitcast(FP8X4),
-                    scales=w_scales[n][:, c, :],
-                    in_=grouped[n][:, c, :, :].rearrange("p o t -> p (o t)"),
-                )
+        def q1(n):
+            w_codes[n] = codes.tile([P, C, NB], U32, name="w_codes", tag="w_codes", align_bytes=64)
+            w_scales[n] = codes.tile([P, C, NB], U8, name="w_scales", tag="w_scales", align_bytes=64)
+            nc.vector.quantize_mx(
+                out=w_codes[n][:].rearrange("p c o -> p (c o)").bitcast(FP8X4),
+                scales=w_scales[n][:].rearrange("p c o -> p (c o)"),
+                in_=grouped[n][:].rearrange("p c o t -> p (c o t)"),
+            )
 
         def MX(n, m):
             acc[n, m] = psum_a.tile([P, NB], F32, name="acc", tag="acc")
@@ -191,35 +209,67 @@ def tile_bitlinear_kernel(tc, x, weight, bias, out):
                     in_=xg[:, c, sl, :].rearrange("p k t -> p (k t)"),
                 )
 
-        for t in range(-28, NBLK * MT):
-            for b in range(NBLK):
-                d = t - MT * b
-                if -28 <= d <= -22 and d % 2 == 0:
-                    S_sum(b, (d + 28) // 2)
-                if d in (-11, -9):
-                    for a in (0, 1) if d == -11 else (2, 3):
-                        T(b, a)
-                        E(b, a)
-            if -20 <= t <= -17:
-                for m in (2 * (t + 20), 2 * (t + 20) + 1):
-                    xT(m)
-                    xc(m)
+        for t in range(HEAD, NBLK * MT):
+            blocks = [(b, t - MT * b) for b in range(NBLK)]
+            h = t - HEAD
+
+            if 0 <= h < A_T:
+                S_sum(0, h)
+            if 0 <= h - HEAD_COPIES < 2:
+                E(0, 2 * (h - HEAD_COPIES))
+                E(0, 2 * (h - HEAD_COPIES) + 1)
+            for b, d in blocks[1:]:
+                if 0 <= d - COPIES < 2:
+                    E(b, 2 * (d - COPIES))
+                    E(b, 2 * (d - COPIES) + 1)
+                if 0 <= d - SUMS < A_T:
+                    S_sum(b, d - SUMS)
+                if sign_scalar(b) and d == SIGNS:
+                    sign(b, 0, A_T)
+
+            if 0 <= h < A_T:
+                xT(2 * h)
+                xT(2 * h + 1)
             j = t + LEAD
             if 0 <= j < NBLK * MT:
                 MX(j // MT, j % MT)
+            if 0 <= h - 5 < 2:
+                T(0, 2 * (h - 5))
+                T(0, 2 * (h - 5) + 1)
+            for b, d in blocks[1:]:
+                if 0 <= d - TURNS < 2:
+                    T(b, 2 * (d - TURNS))
+                    T(b, 2 * (d - TURNS) + 1)
+
             if t >= 0:
                 ev(t // MT, t % MT)
-            if t in (-14, -13):
-                qx(t + 14)
-            for b in range(NBLK):
-                d = t - MT * b
-                if -18 <= d <= -15:
-                    masks(b, d + 18)
-                if -14 <= d <= -11:
-                    prod(b, d + 14)
-                if d in (-6, -5):
-                    q(b, d + 6, d + 7)
-                if -20 <= d <= -17:
-                    sign(b, d + 20)
-                if d == -19:
+            if h == 0:
+                sign(0, 0, 1)
+                xc(0)
+            if 0 <= h < A_T:
+                if h > 0:
+                    xc(2 * h - 1)
+                s2(0, h, h + 1)
+                if h > 0:
+                    xc(2 * h)
+                if h + 1 < A_T:
+                    sign(0, h + 1, h + 2)
+                masks(0, h)
+            if h == A_T:
+                xc(MT - 1)
+            if 0 <= h - 4 < 2:
+                prod2(0, 2 * (h - 4))
+            if 0 <= h - 6 < 2:
+                qx(h - 6)
+            for b, d in blocks[1:]:
+                if d == MASKS - 2:
                     s2(b, 0, A_T)
+                if d == MASKS - 1 and not sign_scalar(b):
+                    sign(b, 0, A_T)
+                if 0 <= d - MASKS < A_T:
+                    masks(b, d - MASKS)
+                if 0 <= d - PRODUCTS < 2:
+                    prod2(b, 2 * (d - PRODUCTS))
+            for b, d in blocks:
+                if d == QUANTISE:
+                    q1(b)

@@ -23,18 +23,28 @@ A_T = NB // P
 G = K // GROUP
 MT = TOK // P
 C = K // 512
-SIGN_SCALAR = (6, 7)
+SIGN_SCALAR = (7,)
 
-SUMS = -29
-SIGNS = -20
-MASKS = -20
+SUMS = -30
+SIGNS = -23
+MASKS = -19
 PRODUCTS = -15
 TURNS = -14
-COPIES = -8
-QUANTISE = -4
+COPIES = -9
+QUANTISE = -6
 LEAD = 3
-HEAD = -29
-HEAD_COPIES = 20
+EARLIER = {}
+TAIL = range(50, 62, 3)
+FOLDED = (2,)
+FOLD_S = 16
+FOLD_J = GROUP // FOLD_S
+TURNED_BLOCKS = (1, 3, 5)
+NT = NB - P
+TURNED = -4
+BACK = 1
+STORE_LAG = 3
+HEAD = -30
+HEAD_COPIES = 22
 
 FLOPS = 2 * TOK * K * OUT
 
@@ -49,7 +59,7 @@ def tile_bitlinear_kernel(tc, x, weight, bias, out):
         work = ctx.enter_context(tc.tile_pool(name="work", bufs=3))
         small = ctx.enter_context(tc.tile_pool(name="small", bufs=4))
         codes = ctx.enter_context(tc.tile_pool(name="codes", bufs=3))
-        outp = ctx.enter_context(tc.tile_pool(name="outp", bufs=8))
+        outp = ctx.enter_context(tc.tile_pool(name="outp", bufs=10))
         psum_t = ctx.enter_context(tc.psum_pool(name="psum_t", bufs=4))
         psum_a = ctx.enter_context(tc.psum_pool(name="psum_a", bufs=4))
         ctx.enter_context(tc.manual_schedule())
@@ -82,6 +92,10 @@ def tile_bitlinear_kernel(tc, x, weight, bias, out):
 
         ident_f = const.tile([P, P], F32, name="ident_f")
         make_identity(nc, ident_f[:])
+        ident_b = const.tile([P, P], BF16, name="ident_b")
+        make_identity(nc, ident_b[:])
+        bias_col = const.tile([P, NBLK], F32, name="bias_col")
+        turned = {}
 
         xg = const.tile([P, C, TOK, 4], BF16, name="xg", align_bytes=64)
         x_codes = const.tile([P, C, TOK], U32, name="x_codes", align_bytes=64)
@@ -97,11 +111,48 @@ def tile_bitlinear_kernel(tc, x, weight, bias, out):
         def alpha(n):
             return 2.0 if sign_scalar(n) else 4.0
 
+        def folded(n):
+            return n in FOLDED
+
+        def turned_block(n):
+            return n in TURNED_BLOCKS
+
+        def new_sums(n):
+            sums[n] = small.tile([P, A_T * G], F32, name="sums", tag="sums")
+            absw[n] = work.tile([P, A_T, K], BF16, name="absw", tag="absw")
+            scales2[n] = small.tile([P, A_T * G], F32, name="s2", tag="s2")
+
+        def pieces(n):
+            return absw[n][:].rearrange("p a k -> p (a k)").rearrange(
+                "p (s h j) -> p s h j", s=FOLD_S, j=FOLD_J
+            )
+
+        def Sabs(n, a):
+            if a == 0:
+                new_sums(n)
+            nc.scalar.activation(
+                out=pieces(n)[:, :, a * G : (a + 1) * G, :],
+                in_=w_sb[n][:, a, :].rearrange("p (g s j) -> p s g j", g=G, j=FOLD_J),
+                func=ACT.Abs,
+                scale=alpha(n),
+            )
+
+        def fold(n):
+            bank["f", n] = psum_t.tile([P, A_T * G, FOLD_J], F32, name="ps_f", tag="tp")
+            for s in range(FOLD_S):
+                nc.tensor.matmul(
+                    bank["f", n][:], lhsT=ident_b[:], rhs=pieces(n)[:, s, :, :],
+                    start=(s == 0), stop=(s == FOLD_S - 1),
+                )
+
+        def red(n):
+            nc.vector.tensor_reduce(
+                out=sums[n][:], in_=bank["f", n][:], axis=mybir.AxisListType.X, op=ALU.add
+            )
+
         def S_sum(n, a):
             if a == 0:
-                sums[n] = small.tile([P, A_T * G], F32, name="sums", tag="sums")
-                absw[n] = work.tile([P, A_T, K], BF16, name="absw", tag="absw")
-                scales2[n] = small.tile([P, A_T * G], F32, name="s2", tag="s2")
+                new_sums(n)
             for g in range(G):
                 j = a * G + g
                 nc.scalar.activation(
@@ -132,17 +183,21 @@ def tile_bitlinear_kernel(tc, x, weight, bias, out):
         def masks(n, a):
             for g in range(G):
                 j = a * G + g
-                sl = absw[n][:, a, g * GROUP : (g + 1) * GROUP]
+                if folded(n):
+                    sl = pieces(n)[:, :, j, :]
+                else:
+                    sl = absw[n][:, a, g * GROUP : (g + 1) * GROUP]
                 nc.vector.tensor_scalar(
                     out=sl, in0=sl, scalar1=scales2[n][:, j : j + 1], scalar2=scales2[n][:, j : j + 1],
                     op0=ALU.is_gt, op1=ALU.mult,
                 )
 
         def prod2(n, a):
-            nc.vector.tensor_tensor(
-                out=sg[n][:, a : a + 2, :], in0=absw[n][:, a : a + 2, :], in1=sg[n][:, a : a + 2, :],
-                op=ALU.mult,
-            )
+            signs, masked = sg[n][:, a : a + 2, :], absw[n][:, a : a + 2, :]
+            if folded(n):
+                signs = signs.rearrange("p a (g s j) -> p (a g) s j", g=G, j=FOLD_J)
+                masked = pieces(n)[:, :, a * G : (a + 2) * G, :].rearrange("p s h j -> p h s j")
+            nc.vector.tensor_tensor(out=signs, in0=masked, in1=signs, op=ALU.mult)
 
         def T(n, a):
             words = sg[n][:].bitcast(F32).rearrange("p a (c q u) -> p a c u q", c=C, u=2)
@@ -168,25 +223,75 @@ def tile_bitlinear_kernel(tc, x, weight, bias, out):
                 in_=grouped[n][:].rearrange("p c o t -> p (c o t)"),
             )
 
-        def MX(n, m):
-            acc[n, m] = psum_a.tile([P, NB], F32, name="acc", tag="acc")
+        def passes(n, out_ap, x0, x1, w0, w1, w_left):
             for c in range(C):
+                xc_, xs_ = x_codes[:, c, x0:x1].bitcast(FP8X4), x_scales[:, c, x0:x1]
+                wc_, ws_ = w_codes[n][:, c, w0:w1].bitcast(FP8X4), w_scales[n][:, c, w0:w1]
+                left, left_s, right, right_s = (wc_, ws_, xc_, xs_) if w_left else (xc_, xs_, wc_, ws_)
                 nc.tensor.matmul_mx(
-                    out=acc[n, m][:],
-                    lhsT=x_codes[:, c, m * P : (m + 1) * P].bitcast(FP8X4),
-                    lhsT_scale=x_scales[:, c, m * P : (m + 1) * P],
-                    rhs=w_codes[n][:, c, :].bitcast(FP8X4),
-                    rhs_scale=w_scales[n][:, c, :],
-                    start=(c == 0),
-                    stop=(c == C - 1),
+                    out=out_ap, lhsT=left, lhsT_scale=left_s, rhs=right, rhs_scale=right_s,
+                    start=(c == 0), stop=(c == C - 1),
                 )
 
+        def MX(n, m):
+            acc[n, m] = psum_a.tile([P, NB], F32, name="acc", tag="acc")
+            for w0, w1 in ((0, 256), (256, NT)) if turned_block(n) else ((0, NB),):
+                passes(n, acc[n, m][:, w0:w1], m * P, (m + 1) * P, w0, w1, False)
+
+        def MXt(n, h):
+            acc["t", n, h] = psum_a.tile([P, 512], F32, name="acc_t", tag="acc")
+            passes(n, acc["t", n, h][:], h * 512, (h + 1) * 512, NT, NB, True)
+
+        def e1(n, h):
+            turned[n, h] = outp.tile([P, 512], F32, name="o_t", tag="o_t", bufs=3)
+            nc.scalar.activation(
+                out=turned[n, h][:], in_=acc["t", n, h][:], func=ACT.Identity,
+                bias=bias_col[:, n : n + 1], scale=1.0,
+            )
+
+        def TB(n, h):
+            bank["o", n, h] = psum_t.tile([P, 4, P], F32, name="ps_o", tag="tp")
+            for j in range(4):
+                nc.tensor.transpose(
+                    bank["o", n, h][:, j, :], turned[n, h][:, j * P : (j + 1) * P], ident_f[:]
+                )
+
+        def e2(n, h):
+            o_b = outp.tile([P, 4, P], F32, name="o_b", tag="o_b", bufs=2)
+            nc.scalar.copy(out=o_b[:], in_=bank["o", n, h][:])
+            nc.sync.dma_start(
+                out=of[h * 512 : (h + 1) * 512, n * NB + NT : (n + 1) * NB].rearrange(
+                    "(j p) o -> p j o", p=P
+                ),
+                in_=o_b[:],
+            )
+
+        def bias_turn():
+            ps = psum_t.tile([P, NBLK, P], BF16, name="ps_b", tag="tp")
+            for n in range(NBLK):
+                nc.tensor.transpose(ps[:, n, :], bias_bc[:, n * NB + NT : (n + 1) * NB], ident_b[:])
+            nc.scalar.copy(out=bias_col[:], in_=ps[:, :, 0])
+
+        waiting = {}
+
         def ev(n, m):
+            nt = NT if turned_block(n) else NB
             o_sb = outp.tile([P, NB], F32, name="o_sb", tag="o_sb")
             nc.vector.tensor_tensor(
-                out=o_sb[:], in0=acc[n, m][:], in1=bias_bc[:, n * NB : (n + 1) * NB], op=ALU.add
+                out=o_sb[:, 0:nt], in0=acc[n, m][:, 0:nt], in1=bias_bc[:, n * NB : n * NB + nt], op=ALU.add
             )
+            nc.sync.dma_start(out=of[m * P : (m + 1) * P, n * NB : n * NB + nt], in_=o_sb[:, 0:nt])
+
+        def store(n, m, o_sb):
             nc.sync.dma_start(out=of[m * P : (m + 1) * P, n * NB : (n + 1) * NB], in_=o_sb[:])
+
+        def ev_scalar(n, m):
+            o_sb = outp.tile([P, NB], F32, name="o_sb", tag="o_sb")
+            nc.scalar.copy(out=o_sb[:], in_=acc[n, m][:])
+            nc.gpsimd.tensor_tensor(
+                out=o_sb[:], in0=o_sb[:], in1=bias_bc[:, n * NB : (n + 1) * NB], op=ALU.add
+            )
+            waiting[n * MT + m] = o_sb
 
         def xT(m):
             bank["x", m] = psum_t.tile([P, C, 2, P], F32, name="ps_x", tag="tp")
@@ -211,6 +316,7 @@ def tile_bitlinear_kernel(tc, x, weight, bias, out):
 
         for t in range(HEAD, NBLK * MT):
             blocks = [(b, t - MT * b) for b in range(NBLK)]
+            early = [(b, d + EARLIER.get(b, 0)) for b, d in blocks]
             h = t - HEAD
 
             if 0 <= h < A_T:
@@ -218,50 +324,79 @@ def tile_bitlinear_kernel(tc, x, weight, bias, out):
             if 0 <= h - HEAD_COPIES < 2:
                 E(0, 2 * (h - HEAD_COPIES))
                 E(0, 2 * (h - HEAD_COPIES) + 1)
-            for b, d in blocks[1:]:
+            for b, d in blocks:
+                if turned_block(b) and 0 <= d - TURNED - 1 < 2:
+                    e1(b, d - TURNED - 1)
+                if turned_block(b) and 0 <= d - BACK - 1 < 2:
+                    e2(b, d - BACK - 1)
+            for b, d in early[1:]:
                 if 0 <= d - COPIES < 2:
                     E(b, 2 * (d - COPIES))
                     E(b, 2 * (d - COPIES) + 1)
+            for b, d in blocks[1:]:
                 if 0 <= d - SUMS < A_T:
-                    S_sum(b, d - SUMS)
+                    if folded(b):
+                        Sabs(b, d - SUMS)
+                    else:
+                        S_sum(b, d - SUMS)
                 if sign_scalar(b) and d == SIGNS:
                     sign(b, 0, A_T)
+            if t in TAIL:
+                ev_scalar(t // MT, t % MT)
 
             if 0 <= h < A_T:
-                xT(2 * h)
-                xT(2 * h + 1)
+                xT(h)
+            if h in (A_T - 1, A_T):
+                xT(2 * h - 2)
+                xT(2 * h - 1)
+            if t == -6:
+                bias_turn()
+            for b, d in blocks:
+                if turned_block(b) and 0 <= d - TURNED < 2:
+                    MXt(b, d - TURNED)
             j = t + LEAD
             if 0 <= j < NBLK * MT:
                 MX(j // MT, j % MT)
-            if 0 <= h - 5 < 2:
-                T(0, 2 * (h - 5))
-                T(0, 2 * (h - 5) + 1)
-            for b, d in blocks[1:]:
+            for b, d in blocks:
+                if turned_block(b) and 0 <= d - BACK < 2:
+                    TB(b, d - BACK)
+            if 0 <= h - 4 < 2:
+                T(0, 2 * (h - 4))
+                T(0, 2 * (h - 4) + 1)
+            for b, d in early[1:]:
                 if 0 <= d - TURNS < 2:
                     T(b, 2 * (d - TURNS))
                     T(b, 2 * (d - TURNS) + 1)
+                if folded(b) and d == SUMS + A_T:
+                    fold(b)
 
-            if t >= 0:
+            if t >= 0 and t not in TAIL:
                 ev(t // MT, t % MT)
+            s = t - STORE_LAG
+            if s in TAIL:
+                store(s // MT, s % MT, waiting[s])
             if h == 0:
                 sign(0, 0, 1)
-                xc(0)
             if 0 <= h < A_T:
-                if h > 0:
-                    xc(2 * h - 1)
+                xc(h)
+                if h == A_T - 1:
+                    prod2(0, 0)
                 s2(0, h, h + 1)
-                if h > 0:
-                    xc(2 * h)
                 if h + 1 < A_T:
                     sign(0, h + 1, h + 2)
                 masks(0, h)
             if h == A_T:
-                xc(MT - 1)
-            if 0 <= h - 4 < 2:
-                prod2(0, 2 * (h - 4))
+                xc(4)
+                xc(5)
+                prod2(0, 2)
+            if h == A_T + 1:
+                xc(6)
+                xc(7)
             if 0 <= h - 6 < 2:
                 qx(h - 6)
-            for b, d in blocks[1:]:
+            for b, d in early[1:]:
+                if d == MASKS - 3 and folded(b):
+                    red(b)
                 if d == MASKS - 2:
                     s2(b, 0, A_T)
                 if d == MASKS - 1 and not sign_scalar(b):
@@ -270,6 +405,6 @@ def tile_bitlinear_kernel(tc, x, weight, bias, out):
                     masks(b, d - MASKS)
                 if 0 <= d - PRODUCTS < 2:
                     prod2(b, 2 * (d - PRODUCTS))
-            for b, d in blocks:
+            for b, d in early:
                 if d == QUANTISE:
                     q1(b)

@@ -34,7 +34,7 @@ COPIES = -9
 QUANTISE = -6
 LEAD = 3
 EARLIER = {}
-TAIL = range(50, 62, 3)
+TAIL = (50, 53)
 FOLDED = (2,)
 FOLD_S = 16
 FOLD_J = GROUP // FOLD_S
@@ -42,6 +42,7 @@ TURNED_BLOCKS = (1, 3, 5)
 NT = NB - P
 TURNED = -4
 BACK = 1
+WIDE = 46
 STORE_LAG = 3
 HEAD = -30
 HEAD_COPIES = 22
@@ -138,7 +139,7 @@ def tile_bitlinear_kernel(tc, x, weight, bias, out):
             )
 
         def fold(n):
-            bank["f", n] = psum_t.tile([P, A_T * G, FOLD_J], F32, name="ps_f", tag="tp")
+            bank["f", n] = psum_a.tile([P, A_T * G, FOLD_J], F32, name="ps_f", tag="acc")
             for s in range(FOLD_S):
                 nc.tensor.matmul(
                     bank["f", n][:], lhsT=ident_b[:], rhs=pieces(n)[:, s, :, :],
@@ -234,7 +235,10 @@ def tile_bitlinear_kernel(tc, x, weight, bias, out):
                 )
 
         def MX(n, m):
-            acc[n, m] = psum_a.tile([P, NB], F32, name="acc", tag="acc")
+            if n * MT + m >= WIDE and m % 2 == 1:
+                acc[n, m] = psum_t.tile([P, NB], F32, name="acc_w", tag="tp")
+            else:
+                acc[n, m] = psum_a.tile([P, NB], F32, name="acc", tag="acc")
             for w0, w1 in ((0, 256), (256, NT)) if turned_block(n) else ((0, NB),):
                 passes(n, acc[n, m][:, w0:w1], m * P, (m + 1) * P, w0, w1, False)
 
@@ -267,7 +271,7 @@ def tile_bitlinear_kernel(tc, x, weight, bias, out):
             )
 
         def bias_turn():
-            ps = psum_t.tile([P, NBLK, P], BF16, name="ps_b", tag="tp")
+            ps = psum_a.tile([P, NBLK, P], BF16, name="ps_b", tag="acc")
             for n in range(NBLK):
                 nc.tensor.transpose(ps[:, n, :], bias_bc[:, n * NB + NT : (n + 1) * NB], ident_b[:])
             nc.scalar.copy(out=bias_col[:], in_=ps[:, :, 0])
@@ -277,10 +281,13 @@ def tile_bitlinear_kernel(tc, x, weight, bias, out):
         def ev(n, m):
             nt = NT if turned_block(n) else NB
             o_sb = outp.tile([P, NB], F32, name="o_sb", tag="o_sb")
-            nc.vector.tensor_tensor(
-                out=o_sb[:, 0:nt], in0=acc[n, m][:, 0:nt], in1=bias_bc[:, n * NB : n * NB + nt], op=ALU.add
-            )
-            nc.sync.dma_start(out=of[m * P : (m + 1) * P, n * NB : n * NB + nt], in_=o_sb[:, 0:nt])
+            last = n == NBLK - 1 and m == MT - 1
+            for c0, c1 in ((0, NB // 2), (NB // 2, NB)) if last else ((0, nt),):
+                cols = slice(n * NB + c0, n * NB + c1)
+                nc.vector.tensor_tensor(
+                    out=o_sb[:, c0:c1], in0=acc[n, m][:, c0:c1], in1=bias_bc[:, cols], op=ALU.add
+                )
+                nc.sync.dma_start(out=of[m * P : (m + 1) * P, cols], in_=o_sb[:, c0:c1])
 
         def store(n, m, o_sb):
             nc.sync.dma_start(out=of[m * P : (m + 1) * P, n * NB : (n + 1) * NB], in_=o_sb[:])

from contextlib import ExitStack

import concourse.mybir as mybir
from concourse.masks import make_identity

F32 = mybir.dt.float32
BF16 = mybir.dt.bfloat16
U32 = mybir.dt.uint32
U8 = mybir.dt.uint8
FP8X4 = mybir.dt.float8_e4m3fn_x4
ALU = mybir.AluOpType
ACT = mybir.ActivationFunctionType

P = 128
TOK = 1024
K = 1024
OUT = 4096
GROUP = 128
EPS = 1e-8
NB = 512
NBLK = OUT // NB
A_T = NB // P
G = K // GROUP
MT = TOK // P
C = K // 512
SIGN_SCALAR = (7,)

SUMS = -30
SIGNS = -23
MASKS = -19
PRODUCTS = -15
TURNS = -14
COPIES = -9
QUANTISE = -6
LEAD = 3
EARLIER = {}
TAIL = (50, 53)
FOLDED = (2,)
FOLD_S = 16
FOLD_J = GROUP // FOLD_S
TURNED_BLOCKS = (1, 3, 5)
NT = NB - P
TURNED = -4
BACK = 1
WIDE = 46
STORE_LAG = 3
HEAD = -30
HEAD_COPIES = 22

FLOPS = 2 * TOK * K * OUT


def tile_bitlinear_kernel(tc, x, weight, bias, out):
    nc = tc.nc
    xf = x.flatten_outer_dims()
    of = out.flatten_outer_dims()
    with ExitStack() as ctx:
        const = ctx.enter_context(tc.tile_pool(name="const", bufs=1))
        wpool = ctx.enter_context(tc.tile_pool(name="wpool", bufs=NBLK))
        work = ctx.enter_context(tc.tile_pool(name="work", bufs=3))
        small = ctx.enter_context(tc.tile_pool(name="small", bufs=4))
        codes = ctx.enter_context(tc.tile_pool(name="codes", bufs=3))
        outp = ctx.enter_context(tc.tile_pool(name="outp", bufs=10))
        psum_t = ctx.enter_context(tc.psum_pool(name="psum_t", bufs=4))
        psum_a = ctx.enter_context(tc.psum_pool(name="psum_a", bufs=4))
        ctx.enter_context(tc.manual_schedule())

        w_sb = []

        def load_w(n):
            w_n = wpool.tile([P, A_T, K], BF16, name="w_n", tag="w_n")
            nc.sync.dma_start(
                out=w_n[:],
                in_=weight[n * NB : (n + 1) * NB, :].rearrange("(a p) k -> p a k", p=P),
            )
            w_sb.append(w_n)

        x_sb = const.tile([P, MT, K], BF16, name="x_sb")
        x_view = xf.rearrange("(m p) k -> p m k", p=P)
        w_0 = wpool.tile([P, A_T, K], BF16, name="w_n", tag="w_n")
        w_sb.append(w_0)
        for m in range(A_T):
            nc.sync.dma_start(out=w_0[:, m, :], in_=weight[m * P : (m + 1) * P, :])
            nc.sync.dma_start(out=x_sb[:, m, :], in_=x_view[:, m, :])
        load_w(1)
        for m in range(A_T, MT):
            nc.sync.dma_start(out=x_sb[:, m, :], in_=x_view[:, m, :])
        load_w(2)
        bias_bc = const.tile([P, OUT], BF16, name="bias_bc")
        nc.sync.dma_start(out=bias_bc[:], in_=bias.partition_broadcast(P))
        for n in range(3, NBLK):
            load_w(n)

        ident_f = const.tile([P, P], F32, name="ident_f")
        make_identity(nc, ident_f[:])
        ident_b = const.tile([P, P], BF16, name="ident_b")
        make_identity(nc, ident_b[:])
        bias_col = const.tile([P, NBLK], F32, name="bias_col")
        turned = {}

        xg = const.tile([P, C, TOK, 4], BF16, name="xg", align_bytes=64)
        x_codes = const.tile([P, C, TOK], U32, name="x_codes", align_bytes=64)
        x_scales = const.tile([P, C, TOK], U8, name="x_scales", align_bytes=64)

        sums, absw, scales2, sg, grouped, w_codes, w_scales, acc, bank = {}, {}, {}, {}, {}, {}, {}, {}, {}
        xw = x_sb[:].bitcast(F32).rearrange("p m (c q u) -> p m c u q", c=C, u=2)
        xg32 = xg[:].bitcast(F32)

        def sign_scalar(n):
            return n in SIGN_SCALAR

        def alpha(n):
            return 2.0 if sign_scalar(n) else 4.0

        def folded(n):
            return n in FOLDED

        def turned_block(n):
            return n in TURNED_BLOCKS

        def new_sums(n):
            sums[n] = small.tile([P, A_T * G], F32, name="sums", tag="sums")
            absw[n] = work.tile([P, A_T, K], BF16, name="absw", tag="absw")
            scales2[n] = small.tile([P, A_T * G], F32, name="s2", tag="s2")

        def pieces(n):
            return absw[n][:].rearrange("p a k -> p (a k)").rearrange(
                "p (s h j) -> p s h j", s=FOLD_S, j=FOLD_J
            )

        def Sabs(n, a):
            if a == 0:
                new_sums(n)
            nc.scalar.activation(
                out=pieces(n)[:, :, a * G : (a + 1) * G, :],
                in_=w_sb[n][:, a, :].rearrange("p (g s j) -> p s g j", g=G, j=FOLD_J),
                func=ACT.Abs,
                scale=alpha(n),
            )

        def fold(n):
            bank["f", n] = psum_a.tile([P, A_T * G, FOLD_J], F32, name="ps_f", tag="acc")
            for s in range(FOLD_S):
                nc.tensor.matmul(
                    bank["f", n][:], lhsT=ident_b[:], rhs=pieces(n)[:, s, :, :],
                    start=(s == 0), stop=(s == FOLD_S - 1),
                )

        def red(n):
            nc.vector.tensor_reduce(
                out=sums[n][:], in_=bank["f", n][:], axis=mybir.AxisListType.X, op=ALU.add
            )

        def S_sum(n, a):
            if a == 0:
                new_sums(n)
            for g in range(G):
                j = a * G + g
                nc.scalar.activation(
                    out=absw[n][:, a, g * GROUP : (g + 1) * GROUP],
                    in_=w_sb[n][:, a, g * GROUP : (g + 1) * GROUP],
                    func=ACT.Abs,
                    scale=alpha(n),
                    accum_out=sums[n][:, j : j + 1],
                )

        def sign(n, a0, a1):
            if a0 == 0:
                sg[n] = work.tile([P, A_T, K], BF16, name="sg", tag="sg")
            if sign_scalar(n):
                nc.scalar.activation(out=sg[n][:, a0:a1, :], in_=w_sb[n][:, a0:a1, :], func=ACT.Sign)
            else:
                nc.vector.tensor_scalar(
                    out=sg[n][:, a0:a1, :], in0=w_sb[n][:, a0:a1, :],
                    scalar1=0.0, scalar2=0.5, op0=ALU.is_ge, op1=ALU.subtract,
                )

        def s2(n, a0, a1):
            nc.vector.tensor_scalar(
                out=scales2[n][:, a0 * G : a1 * G], in0=sums[n][:, a0 * G : a1 * G],
                scalar1=1.0 / 256.0, scalar2=EPS * alpha(n) / 2, op0=ALU.mult, op1=ALU.max,
            )

        def masks(n, a):
            for g in range(G):
                j = a * G + g
                if folded(n):
                    sl = pieces(n)[:, :, j, :]
                else:
                    sl = absw[n][:, a, g * GROUP : (g + 1) * GROUP]
                nc.vector.tensor_scalar(
                    out=sl, in0=sl, scalar1=scales2[n][:, j : j + 1], scalar2=scales2[n][:, j : j + 1],
                    op0=ALU.is_gt, op1=ALU.mult,
                )

        def prod2(n, a):
            signs, masked = sg[n][:, a : a + 2, :], absw[n][:, a : a + 2, :]
            if folded(n):
                signs = signs.rearrange("p a (g s j) -> p (a g) s j", g=G, j=FOLD_J)
                masked = pieces(n)[:, :, a * G : (a + 2) * G, :].rearrange("p s h j -> p h s j")
            nc.vector.tensor_tensor(out=signs, in0=masked, in1=signs, op=ALU.mult)

        def T(n, a):
            words = sg[n][:].bitcast(F32).rearrange("p a (c q u) -> p a c u q", c=C, u=2)
            bank["w", n, a] = psum_t.tile([P, C, 2, P], F32, name="ps_w", tag="tp")
            for c in range(C):
                for u in range(2):
                    nc.tensor.transpose(bank["w", n, a][:, c, u, :], words[:, a, c, u, :], ident_f[:])

        def E(n, a):
            if a == 0:
                grouped[n] = work.tile([P, C, NB, 4], BF16, name="grouped", tag="grouped", bufs=2, align_bytes=64)
            nc.scalar.copy(
                out=grouped[n][:].bitcast(F32)[:, :, a * P : (a + 1) * P, :],
                in_=bank["w", n, a][:].rearrange("p c u o -> p c o u"),
            )

        def q1(n):
            w_codes[n] = codes.tile([P, C, NB], U32, name="w_codes", tag="w_codes", align_bytes=64)
            w_scales[n] = codes.tile([P, C, NB], U8, name="w_scales", tag="w_scales", align_bytes=64)
            nc.vector.quantize_mx(
                out=w_codes[n][:].rearrange("p c o -> p (c o)").bitcast(FP8X4),
                scales=w_scales[n][:].rearrange("p c o -> p (c o)"),
                in_=grouped[n][:].rearrange("p c o t -> p (c o t)"),
            )

        def passes(n, out_ap, x0, x1, w0, w1, w_left):
            for c in range(C):
                xc_, xs_ = x_codes[:, c, x0:x1].bitcast(FP8X4), x_scales[:, c, x0:x1]
                wc_, ws_ = w_codes[n][:, c, w0:w1].bitcast(FP8X4), w_scales[n][:, c, w0:w1]
                left, left_s, right, right_s = (wc_, ws_, xc_, xs_) if w_left else (xc_, xs_, wc_, ws_)
                nc.tensor.matmul_mx(
                    out=out_ap, lhsT=left, lhsT_scale=left_s, rhs=right, rhs_scale=right_s,
                    start=(c == 0), stop=(c == C - 1),
                )

        def MX(n, m):
            if n * MT + m >= WIDE and m % 2 == 1:
                acc[n, m] = psum_t.tile([P, NB], F32, name="acc_w", tag="tp")
            else:
                acc[n, m] = psum_a.tile([P, NB], F32, name="acc", tag="acc")
            for w0, w1 in ((0, 256), (256, NT)) if turned_block(n) else ((0, NB),):
                passes(n, acc[n, m][:, w0:w1], m * P, (m + 1) * P, w0, w1, False)

        def MXt(n, h):
            acc["t", n, h] = psum_a.tile([P, 512], F32, name="acc_t", tag="acc")
            passes(n, acc["t", n, h][:], h * 512, (h + 1) * 512, NT, NB, True)

        def e1(n, h):
            turned[n, h] = outp.tile([P, 512], F32, name="o_t", tag="o_t", bufs=3)
            nc.scalar.activation(
                out=turned[n, h][:], in_=acc["t", n, h][:], func=ACT.Identity,
                bias=bias_col[:, n : n + 1], scale=1.0,
            )

        def TB(n, h):
            bank["o", n, h] = psum_t.tile([P, 4, P], F32, name="ps_o", tag="tp")
            for j in range(4):
                nc.tensor.transpose(
                    bank["o", n, h][:, j, :], turned[n, h][:, j * P : (j + 1) * P], ident_f[:]
                )

        def e2(n, h):
            o_b = outp.tile([P, 4, P], F32, name="o_b", tag="o_b", bufs=2)
            nc.scalar.copy(out=o_b[:], in_=bank["o", n, h][:])
            nc.sync.dma_start(
                out=of[h * 512 : (h + 1) * 512, n * NB + NT : (n + 1) * NB].rearrange(
                    "(j p) o -> p j o", p=P
                ),
                in_=o_b[:],
            )

        def bias_turn():
            ps = psum_a.tile([P, NBLK, P], BF16, name="ps_b", tag="acc")
            for n in range(NBLK):
                nc.tensor.transpose(ps[:, n, :], bias_bc[:, n * NB + NT : (n + 1) * NB], ident_b[:])
            nc.scalar.copy(out=bias_col[:], in_=ps[:, :, 0])

        waiting = {}

        def ev(n, m):
            nt = NT if turned_block(n) else NB
            o_sb = outp.tile([P, NB], F32, name="o_sb", tag="o_sb")
            last = n == NBLK - 1 and m == MT - 1
            for c0, c1 in ((0, NB // 2), (NB // 2, NB)) if last else ((0, nt),):
                cols = slice(n * NB + c0, n * NB + c1)
                nc.vector.tensor_tensor(
                    out=o_sb[:, c0:c1], in0=acc[n, m][:, c0:c1], in1=bias_bc[:, cols], op=ALU.add
                )
                nc.sync.dma_start(out=of[m * P : (m + 1) * P, cols], in_=o_sb[:, c0:c1])

        def store(n, m, o_sb):
            nc.sync.dma_start(out=of[m * P : (m + 1) * P, n * NB : (n + 1) * NB], in_=o_sb[:])

        def ev_scalar(n, m):
            o_sb = outp.tile([P, NB], F32, name="o_sb", tag="o_sb")
            nc.scalar.copy(out=o_sb[:], in_=acc[n, m][:])
            nc.gpsimd.tensor_tensor(
                out=o_sb[:], in0=o_sb[:], in1=bias_bc[:, n * NB : (n + 1) * NB], op=ALU.add
            )
            waiting[n * MT + m] = o_sb

        def xT(m):
            bank["x", m] = psum_t.tile([P, C, 2, P], F32, name="ps_x", tag="tp")
            for c in range(C):
                for u in range(2):
                    nc.tensor.transpose(bank["x", m][:, c, u, :], xw[:, m, c, u, :], ident_f[:])

        def xc(m):
            nc.vector.tensor_copy(
                out=xg32[:, :, m * P : (m + 1) * P, :],
                in_=bank["x", m][:].rearrange("p c u k -> p c k u"),
            )

        def qx(h):
            sl = slice(h * 512, (h + 1) * 512)
            for c in range(C):
                nc.vector.quantize_mx(
                    out=x_codes[:, c, sl].bitcast(FP8X4),
                    scales=x_scales[:, c, sl],
                    in_=xg[:, c, sl, :].rearrange("p k t -> p (k t)"),
                )

        for t in range(HEAD, NBLK * MT):
            blocks = [(b, t - MT * b) for b in range(NBLK)]
            early = [(b, d + EARLIER.get(b, 0)) for b, d in blocks]
            h = t - HEAD

            if 0 <= h < A_T:
                S_sum(0, h)
            if 0 <= h - HEAD_COPIES < 2:
                E(0, 2 * (h - HEAD_COPIES))
                E(0, 2 * (h - HEAD_COPIES) + 1)
            for b, d in blocks:
                if turned_block(b) and 0 <= d - TURNED - 1 < 2:
                    e1(b, d - TURNED - 1)
                if turned_block(b) and 0 <= d - BACK - 1 < 2:
                    e2(b, d - BACK - 1)
            for b, d in early[1:]:
                if 0 <= d - COPIES < 2:
                    E(b, 2 * (d - COPIES))
                    E(b, 2 * (d - COPIES) + 1)
            for b, d in blocks[1:]:
                if 0 <= d - SUMS < A_T:
                    if folded(b):
                        Sabs(b, d - SUMS)
                    else:
                        S_sum(b, d - SUMS)
                if sign_scalar(b) and d == SIGNS:
                    sign(b, 0, A_T)
            if t in TAIL:
                ev_scalar(t // MT, t % MT)

            if 0 <= h < A_T:
                xT(h)
            if h in (A_T - 1, A_T):
                xT(2 * h - 2)
                xT(2 * h - 1)
            if t == -6:
                bias_turn()
            for b, d in blocks:
                if turned_block(b) and 0 <= d - TURNED < 2:
                    MXt(b, d - TURNED)
            j = t + LEAD
            if 0 <= j < NBLK * MT:
                MX(j // MT, j % MT)
            for b, d in blocks:
                if turned_block(b) and 0 <= d - BACK < 2:
                    TB(b, d - BACK)
            if 0 <= h - 4 < 2:
                T(0, 2 * (h - 4))
                T(0, 2 * (h - 4) + 1)
            for b, d in early[1:]:
                if 0 <= d - TURNS < 2:
                    T(b, 2 * (d - TURNS))
                    T(b, 2 * (d - TURNS) + 1)
                if folded(b) and d == SUMS + A_T:
                    fold(b)

            if t >= 0 and t not in TAIL:
                ev(t // MT, t % MT)
            s = t - STORE_LAG
            if s in TAIL:
                store(s // MT, s % MT, waiting[s])
            if h == 0:
                sign(0, 0, 1)
            if 0 <= h < A_T:
                xc(h)
                if h == A_T - 1:
                    prod2(0, 0)
                s2(0, h, h + 1)
                if h + 1 < A_T:
                    sign(0, h + 1, h + 2)
                masks(0, h)
            if h == A_T:
                xc(4)
                xc(5)
                prod2(0, 2)
            if h == A_T + 1:
                xc(6)
                xc(7)
            if 0 <= h - 6 < 2:
                qx(h - 6)
            for b, d in early[1:]:
                if d == MASKS - 3 and folded(b):
                    red(b)
                if d == MASKS - 2:
                    s2(b, 0, A_T)
                if d == MASKS - 1 and not sign_scalar(b):
                    sign(b, 0, A_T)
                if 0 <= d - MASKS < A_T:
                    masks(b, d - MASKS)
                if 0 <= d - PRODUCTS < 2:
                    prod2(b, 2 * (d - PRODUCTS))
            for b, d in early:
                if d == QUANTISE:
                    q1(b)
